import numpy as np
import ml_dtypes


def mxq(x, axis, fmt="e4m3"):
    dtype, down = {"e4m3": (ml_dtypes.float8_e4m3fn, 7), "e5m2": (ml_dtypes.float8_e5m2, 14)}[fmt]
    v = np.moveaxis(np.asarray(x, np.float32).astype(ml_dtypes.bfloat16).astype(np.float64), axis, -1)
    blocks = v.reshape(v.shape[:-1] + (-1, 32))
    amax = np.abs(blocks).max(-1, keepdims=True)
    byte = np.maximum(np.where(amax > 0, np.frexp(amax)[1] - 1 + 127, 0) - down, 1)
    scale = np.exp2(byte - 127.0)
    codes = (blocks / scale).astype(np.float32).astype(dtype).astype(np.float64)
    return np.moveaxis((codes * scale).reshape(v.shape), -1, axis)


WIDE = False


def mx_kscale(k):
    if not WIDE:
        return np.ones(k)
    levels = np.array([10, -10, 5, -5, 0])
    if k % 512:
        return np.exp2(np.random.permutation(np.resize(levels, k // 32))).repeat(32)
    a = np.empty((k // 512, 16))
    for p in range(k // 512):
        a[p, :8] = np.random.permutation(np.resize(levels, 8))
        for g in range(8):
            far = levels[np.abs(levels - a[p, g]) >= 10]
            a[p, g + 8] = far[np.random.randint(len(far))]
    return np.exp2(a.ravel()).repeat(32)


BF16 = ml_dtypes.bfloat16


def bf(x):
    return np.asarray(x, np.float32).astype(BF16)


def f64(x):
    return np.asarray(x).astype(np.float64)


B, S, E, H, HKV, D, F, M0, M1 = 1, 512, 1536, 32, 4, 128, 8192, 48, 40
M2 = D - M0 - M1
ROPE_BASE = 1000000.0
EPS = 1e-6


def rms_norm(v, w):
    return w * (v / np.sqrt(np.mean(v * v, axis=-1, keepdims=True) + EPS))


def mrope_cos_sin():
    t = np.arange(S, dtype=np.float64)
    parts = []
    for sd in (M0, M1, M2):
        inv_freq = 1.0 / ROPE_BASE ** (np.arange(0, sd, 2, dtype=np.float64) / sd)
        freqs = t[:, None] * inv_freq[None, :]
        parts.append(np.concatenate([freqs, freqs], -1))
    emb = np.concatenate(parts, -1)
    return np.cos(emb), np.sin(emb)


def rotate_half(v):
    d = D // 2
    return np.concatenate([-v[..., d:], v[..., :d]], -1)


def setup_inputs():
    s = mx_kscale(E)
    row = 0.5 + 1.5 * np.random.random_sample((B, S, 1))
    return {"x": bf(np.random.standard_normal((B, S, E)) * row),
            "ln1_w": bf((1.0 + 0.1 * np.random.standard_normal(E)) * s),
            "wq": bf(np.random.standard_normal((H * D, E)) / np.sqrt(E) / s),
            "wk": bf(np.random.standard_normal((HKV * D, E)) / np.sqrt(E) / s),
            "wv": bf(np.random.standard_normal((HKV * D, E)) / np.sqrt(E) / s),
            "q_norm_w": bf(1.0 + 0.1 * np.random.standard_normal(D)),
            "k_norm_w": bf(1.0 + 0.1 * np.random.standard_normal(D))}


def reference(x, ln1_w, wq, wk, wv, q_norm_w, k_norm_w):
    hq = mxq(rms_norm(f64(x), f64(ln1_w)), 2, "e4m3")
    q = (hq @ mxq(f64(wq), 1, "e4m3").T).reshape(B, S, H, D).transpose(0, 2, 1, 3)
    k = (hq @ mxq(f64(wk), 1, "e4m3").T).reshape(B, S, HKV, D).transpose(0, 2, 1, 3)
    v = (hq @ mxq(f64(wv), 1, "e4m3").T).reshape(B, S, HKV, D).transpose(0, 2, 1, 3)
    q = rms_norm(q, f64(q_norm_w))
    k = rms_norm(k, f64(k_norm_w))
    cos, sin = mrope_cos_sin()
    q = q * cos + rotate_half(q) * sin
    k = k * cos + rotate_half(k) * sin
    return q, k, v

@@ -1,0 +1,537 @@
+import math
+from contextlib import ExitStack
+
+import concourse.mybir as mybir
+from concourse.masks import make_identity
+
+F32 = mybir.dt.float32
+BF16 = mybir.dt.bfloat16
+I32 = mybir.dt.int32
+U32 = mybir.dt.uint32
+U8 = mybir.dt.uint8
+FP8X4 = mybir.dt.float8_e4m3fn_x4
+ACT = mybir.ActivationFunctionType
+ALU = mybir.AluOpType
+
+P = 128
+S = 512
+E = 1536
+D = 128
+NA = S // P
+NG = E // 512
+NC = 10
+NF = 44
+ROPE_BASE = 1000000.0
+EPS = 1e-6
+TWO_PI = 2.0 * math.pi
+RAW_BUFS = 5
+MANUAL = True
+
+FLOPS = 2 * S * E * (NC * 512)
+
+
+def tile_selectivetransformerlayer_pa_kernel(
+    tc, x, ln1_w, wq, wk, wv, q_norm_w, k_norm_w, out_0, out_1, out_2
+):
+    nc = tc.nc
+    with ExitStack() as ctx:
+        const = ctx.enter_context(tc.tile_pool(name="const", bufs=1))
+        rawp = ctx.enter_context(tc.tile_pool(name="rawp", bufs=RAW_BUFS))
+        codep = ctx.enter_context(tc.tile_pool(name="codep", bufs=3))
+        grp = ctx.enter_context(tc.tile_pool(name="grp", bufs=3))
+        small = ctx.enter_context(tc.tile_pool(name="small", bufs=4))
+        ep = ctx.enter_context(tc.tile_pool(name="ep", bufs=3))
+        outp = ctx.enter_context(tc.tile_pool(name="outp", bufs=4))
+        psum_t = ctx.enter_context(tc.psum_pool(name="psum_t", bufs=4))
+        psum_a = ctx.enter_context(tc.psum_pool(name="psum_a", bufs=4))
+        if MANUAL:
+            ctx.enter_context(tc.manual_schedule())
+
+        x_v = x.rearrange("o (p a) k -> p (o a) k", a=NA)
+        wq_v = wq.rearrange("(c b p) k -> c p b k", b=4, p=P)
+        wk_v = wk.rearrange("(b p) k -> p b k", p=P)
+        wv_v = wv.rearrange("(b p) k -> p b k", p=P)
+        o0_v = out_0.rearrange("o h (p a) d -> p (o h) (a d)", a=NA)
+        o1_v = out_1.rearrange("o h (p a) d -> p (o h) (a d)", a=NA)
+        o2_v = out_2.rearrange("o h (p a) d -> p (o h) (a d)", a=NA)
+
+        def w_src(c):
+            if c == NC - 1:
+                return wv_v
+            if c == NC - 2:
+                return wk_v
+            return wq_v[c]
+
+        def o_dst(c, a0, a1):
+            cols = slice(a0 * D, a1 * D)
+            if c == NC - 1:
+                return o2_v[:, :, cols]
+            if c == NC - 2:
+                return o1_v[:, :, cols]
+            return o0_v[:, 4 * c : 4 * c + 4, cols]
+
+        wrow = const.tile([P, E + 2 * D], BF16)
+        nc.vector.memset(wrow[:], 0.0)
+        ones_b = const.tile([P, P], BF16)
+        nc.vector.memset(ones_b[:], 1.0)
+        warm = const.tile([P, 1], F32)
+        nc.vector.memset(warm[:], 0.0)
+        eps_t = const.tile([P, 1], F32)
+        nc.vector.memset(eps_t[:], EPS)
+        neghalf = const.tile([P, 1], F32)
+        nc.vector.memset(neghalf[:], -0.5)
+
+        x_sb = const.tile([P, NA, E], BF16)
+        for a in range(2):
+            nc.sync.dma_start(out=x_sb[:, a, :], in_=x_v[:, a, :])
+        nc.sync.dma_start(out=wrow[0:1, 0:E], in_=ln1_w.unsqueeze(0))
+        nc.sync.dma_start(out=wrow[0:1, E : E + D], in_=q_norm_w.unsqueeze(0))
+        nc.sync.dma_start(out=wrow[0:1, E + D : E + 2 * D], in_=k_norm_w.unsqueeze(0))
+        for a in range(2, NA):
+            nc.sync.dma_start(out=x_sb[:, a, :], in_=x_v[:, a, :])
+
+        raw = {}
+
+        def load_w(c):
+            w_raw = rawp.tile([P, 4, E], BF16, tag="w_raw")
+            nc.sync.dma_start(out=w_raw[:], in_=w_src(c))
+            raw[c] = w_raw
+
+        for c in range(RAW_BUFS):
+            load_w(c)
+
+        tpos_i = const.tile([P, NA], I32)
+        nc.gpsimd.iota(tpos_i[:], pattern=[[1, NA]], base=0, channel_multiplier=NA)
+        ident_f = const.tile([P, P], F32)
+        make_identity(nc, ident_f[:])
+        ident_b = const.tile([P, P], BF16)
+        make_identity(nc, ident_b[:])
+        warm2 = const.tile([P, 1], F32)
+        nc.scalar.activation(out=warm2[:], in_=warm[:], func=ACT.Sin)
+
+        tpos = const.tile([P, NA], F32)
+        nc.vector.tensor_copy(out=tpos[:], in_=tpos_i[:])
+        turns = const.tile([P, 2, NF, NA], F32)
+        for j in range(NF):
+            if j < 24:
+                cj = ROPE_BASE ** (-2.0 * j / 48.0) / TWO_PI
+            else:
+                cj = ROPE_BASE ** (-2.0 * (j - 24) / 40.0) / TWO_PI
+            nc.vector.tensor_scalar_mul(out=turns[:, 1, j, :], in0=tpos[:], scalar1=cj)
+        nc.vector.tensor_scalar_add(out=turns[:, 0], in0=turns[:, 1], scalar1=0.25)
+        NT = 2 * NF * NA
+        turns_f = turns[:].rearrange("p s j a -> p (s j a)")
+        whole_i = const.tile([P, NT], I32)
+        nc.vector.tensor_copy(out=whole_i[:], in_=turns_f)
+        whole = const.tile([P, NT], F32)
+        nc.vector.tensor_copy(out=whole[:], in_=whole_i[:])
+        frac = const.tile([P, NT], F32)
+        nc.vector.tensor_tensor(out=frac[:], in0=turns_f, in1=whole[:], op=ALU.subtract)
+        fneg = const.tile([P, NT], F32)
+        nc.vector.scalar_tensor_tensor(
+            out=fneg[:], in0=frac[:], scalar=0.5, in1=frac[:], op0=ALU.is_gt, op1=ALU.subtract
+        )
+        fr = const.tile([P, 2, NF, NA], F32)
+        nc.vector.scalar_tensor_tensor(
+            out=fr[:].rearrange("p s j a -> p (s j a)"),
+            in0=fneg[:],
+            scalar=0.5,
+            in1=fneg[:],
+            op0=ALU.is_gt,
+            op1=ALU.subtract,
+        )
+
+        wb = []
+        for i in range(4):
+            n = 512 if i < 3 else 2 * D
+            wbi = psum_a.tile([P, 512], F32, tag="acc", name="wb%d" % i)
+            nc.tensor.matmul(
+                out=wbi[:, 0:n], lhsT=ones_b[:], rhs=wrow[:, 512 * i : 512 * i + n], start=True, stop=True
+            )
+            wb.append(wbi)
+        wqk = const.tile([P, 2 * D], F32)
+        nc.vector.tensor_copy(out=wqk[:], in_=wb[3][:, 0 : 2 * D])
+
+        h = const.tile([P, NA, E], BF16)
+        junk = const.tile([P, E], BF16)
+        ssx = const.tile([P, NA], F32)
+        msx = const.tile([P, NA], F32)
+        rx = const.tile([P, NA], F32)
+        h_codes = const.tile([P, NG, S], U32, align_bytes=64)
+        h_scales = const.tile([P, NG, S], U8, align_bytes=64)
+
+        def x_square(a):
+            nc.scalar.activation(
+                out=junk[:], in_=x_sb[:, a, :], func=ACT.Square, accum_out=ssx[:, a : a + 1]
+            )
+            nc.gpsimd.tensor_scalar(
+                out=msx[:, a : a + 1],
+                in0=ssx[:, a : a + 1],
+                scalar1=1.0 / E,
+                scalar2=EPS,
+                op0=ALU.mult,
+                op1=ALU.add,
+            )
+            nc.gpsimd.tensor_tensor(
+                out=rx[:, a : a + 1], in0=msx[:, a : a + 1], in1=neghalf[:], op=ALU.pow
+            )
+
+        def h_make(a):
+            for g in range(NG):
+                sl = slice(g * 512, (g + 1) * 512)
+                nc.vector.scalar_tensor_tensor(
+                    out=h[:, a, sl].rearrange("p (t q) -> p t q", t=4),
+                    in0=x_sb[:, a, sl].rearrange("p (q t) -> p t q", t=4),
+                    scalar=rx[:, a : a + 1],
+                    in1=wb[g][:].rearrange("p (q t) -> p t q", t=4),
+                    op0=ALU.mult,
+                    op1=ALU.mult,
+                )
+
+        hts = {}
+        hgs = {}
+
+        def h_transpose(pr):
+            for g in range(NG):
+                ht = psum_t.tile([P, 2, 4, P], BF16, tag="tp")
+                for i in range(2):
+                    for t4 in range(4):
+                        lo = (4 * g + t4) * P
+                        nc.tensor.transpose(ht[:, i, t4, :], h[:, 2 * pr + i, lo : lo + P], ident_b[:])
+                hts[(pr, g)] = ht
+
+        def h_copy(pr, g, eng):
+            hg = grp.tile([P, 2, P, 4], BF16, tag="hg", align_bytes=64)
+            src = hts[(pr, g)][:].rearrange("p i t r -> p i r t")
+            if eng == "s":
+                nc.scalar.copy(out=hg[:], in_=src)
+            else:
+                nc.vector.tensor_copy(out=hg[:], in_=src)
+            hgs[(pr, g)] = hg
+
+        def h_quant(pr, g):
+            cols = slice(pr * 256, (pr + 1) * 256)
+            nc.vector.quantize_mx(
+                out=h_codes[:, g, cols].bitcast(FP8X4),
+                scales=h_scales[:, g, cols],
+                in_=hgs[(pr, g)][:].rearrange("p i r t -> p (i r t)"),
+            )
+
+        cos_t = const.tile([P, NA, D], F32)
+        sin_t = const.tile([P, NA, D], F32)
+        tabs = {}
+
+        def sin_tables():
+            pieces = (
+                (cos_t, 0, 0, 48, 0, 24, 2, 1.0),
+                (cos_t, 0, 48, 128, 24, 44, 4, 1.0),
+                (sin_t, 1, 0, 48, 0, 24, 2, -1.0),
+                (sin_t, 1, 48, 64, 24, 40, 1, -1.0),
+                (sin_t, 1, 64, 68, 40, 44, 1, 1.0),
+                (sin_t, 1, 68, 128, 24, 44, 3, 1.0),
+            )
+            for dst, s, d0, d1, j0, j1, r, sign in pieces:
+                nc.scalar.activation(
+                    out=dst[:, :, d0:d1].rearrange("p a (r j) -> p a r j", r=r),
+                    in_=fr[:, s, j0:j1, :]
+                    .rearrange("p j a -> p a j")
+                    .unsqueeze(2)
+                    .to_broadcast([P, NA, r, j1 - j0]),
+                    func=ACT.Sin,
+                    scale=sign * TWO_PI,
+                )
+
+        def w_tables():
+            for i, nm in enumerate(("q", "k")):
+                tab = const.tile([P, NA, 2, D], F32, name="tab_" + nm)
+                ta = tab[:, :, 0, :]
+                tb = tab[:, :, 1, :]
+                w0 = i * D
+                nc.gpsimd.tensor_tensor(
+                    out=ta,
+                    in0=cos_t[:],
+                    in1=wqk[:, w0 : w0 + D].unsqueeze(1).to_broadcast([P, NA, D]),
+                    op=ALU.mult,
+                )
+                nc.gpsimd.tensor_tensor(
+                    out=tb[:, :, 0:64],
+                    in0=sin_t[:, :, 64:128],
+                    in1=wqk[:, w0 : w0 + 64].unsqueeze(1).to_broadcast([P, NA, 64]),
+                    op=ALU.mult,
+                )
+                nc.gpsimd.tensor_tensor(
+                    out=tb[:, :, 64:128],
+                    in0=sin_t[:, :, 0:64],
+                    in1=wqk[:, w0 + 64 : w0 + D].unsqueeze(1).to_broadcast([P, NA, 64]),
+                    op=ALU.mult,
+                )
+                tabs[nm] = tab
+
+        wts = {}
+        wgs = {}
+        wcodes = {}
+
+        def w_transpose(unit):
+            c, g, bp = unit // 6, (unit % 6) // 2, unit % 2
+            wt = psum_t.tile([P, 2, 256], F32, tag="tp")
+            for bl in range(2):
+                for u in range(2):
+                    lo = 256 * g + u
+                    nc.tensor.transpose(
+                        wt[:, u, bl * P : (bl + 1) * P],
+                        raw[c][:, 2 * bp + bl, :].bitcast(F32)[:, lo : 256 * (g + 1) : 2],
+                        ident_f[:],
+                    )
+            wts[unit] = wt
+
+        def w_copy(unit, eng):
+            bp = unit % 2
+            if bp == 0:
+                wg = grp.tile([P, 2048], BF16, tag="wg", align_bytes=64)
+                wgs[unit // 2] = wg
+            wg32 = wgs[unit // 2][:].bitcast(F32).rearrange("p (n u) -> p n u", u=2)
+            dst = wg32[:, bp * 256 : (bp + 1) * 256, :]
+            src = wts[unit][:].rearrange("p u n -> p n u")
+            if eng == "s":
+                nc.scalar.copy(out=dst, in_=src)
+            else:
+                nc.vector.tensor_copy(out=dst, in_=src)
+
+        def w_quant(tile_no):
+            c, g = tile_no // 3, tile_no % 3
+            if g == 0:
+                codes = codep.tile([P, NG, 512], U32, tag="codes", align_bytes=64)
+                scales = codep.tile([P, NG, 512], U8, tag="scales", align_bytes=64)
+                wcodes[c] = (codes, scales)
+            codes, scales = wcodes[c]
+            nc.vector.quantize_mx(
+                out=codes[:, g, :].bitcast(FP8X4), scales=scales[:, g, :], in_=wgs[tile_no][:]
+            )
+
+        accs = {}
+        rss = {}
+        prods = {}
+
+        def mx(slot):
+            c, a = slot // NA, slot % NA
+            codes, scales = wcodes[c]
+            acc = psum_a.tile([P, 512], F32, tag="acc")
+            for g in range(NG):
+                nc.tensor.matmul_mx(
+                    out=acc[:],
+                    lhsT=h_codes[:, g, a * P : (a + 1) * P].bitcast(FP8X4),
+                    lhsT_scale=h_scales[:, g, a * P : (a + 1) * P],
+                    rhs=codes[:, g, :].bitcast(FP8X4),
+                    rhs_scale=scales[:, g, :],
+                    start=(g == 0),
+                    stop=(g == NG - 1),
+                )
+            accs[slot] = acc
+
+        sss = {}
+
+        def head_squares(slot):
+            acc = accs[slot]
+            ss = small.tile([P, 4], F32, tag="ss")
+            sss[slot] = ss
+            for hh in range(4):
+                sq = small.tile([P, D], BF16, tag="sq")
+                nc.scalar.activation(
+                    out=sq[:],
+                    in_=acc[:, hh * D : (hh + 1) * D],
+                    func=ACT.Square,
+                    accum_out=ss[:, hh : hh + 1],
+                )
+
+        def head_rsqrt(slot):
+            rs = small.tile([P, 4], F32, tag="rs")
+            nc.scalar.activation(
+                out=rs[:], in_=sss[slot][:], func=ACT.Abs_reciprocal_sqrt, scale=1.0 / D, bias=eps_t[:]
+            )
+            rss[slot] = rs
+
+        def rope_products(slot):
+            c, a = slot // NA, slot % NA
+            acc = accs[slot]
+            rs = rss[slot]
+            tab = tabs["k" if c == NC - 2 else "q"]
+            if slot % 2 == 0:
+                t12 = ep.tile([P, 4, 2, 2, D], F32, tag="t12")
+                prods[slot // 2] = t12
+            t12 = prods[slot // 2]
+            for hh in range(4):
+                nc.vector.scalar_tensor_tensor(
+                    out=t12[:, hh, slot % 2, :, :],
+                    in0=acc[:, hh * D : (hh + 1) * D].unsqueeze(1).to_broadcast([P, 2, D]),
+                    scalar=rs[:, hh : hh + 1],
+                    in1=tab[:, a, :, :],
+                    op0=ALU.mult,
+                    op1=ALU.mult,
+                )
+
+        outs = {}
+
+        def out_tile(pair):
+            o = outp.tile([P, 4, 2, D], F32, tag="o")
+            outs[pair] = o
+
+        def rope_add(pair, i0, i1, eng):
+            t12 = prods[pair]
+            o = outs[pair]
+            eng.tensor_tensor(
+                out=o[:, :, i0:i1, 0:64],
+                in0=t12[:, :, i0:i1, 0, 0:64],
+                in1=t12[:, :, i0:i1, 1, 64:128],
+                op=ALU.add,
+            )
+            eng.tensor_tensor(
+                out=o[:, :, i0:i1, 64:128],
+                in0=t12[:, :, i0:i1, 0, 64:128],
+                in1=t12[:, :, i0:i1, 1, 0:64],
+                op=ALU.add,
+            )
+
+        def store(pair, i0, i1):
+            c, a = (2 * pair) // NA, (2 * pair) % NA
+            src = outs[pair]
+            if i1 - i0 == 2:
+                nc.sync.dma_start(out=o_dst(c, a, a + 2), in_=src[:].rearrange("p h i d -> p h (i d)"))
+            else:
+                nc.sync.dma_start(out=o_dst(c, a + i0, a + i1), in_=src[:, :, i0, :])
+
+        def v_copy(slot, eng):
+            dst = outs[slot // 2][:, :, slot % 2, :]
+            src = accs[slot][:].rearrange("p (h d) -> p h d", d=D)
+            if eng == "s":
+                nc.scalar.copy(out=dst, in_=src)
+            else:
+                nc.vector.tensor_copy(out=dst, in_=src)
+
+        def t_units(units):
+            for unit in units:
+                w_transpose(unit)
+                if unit % 6 == 5 and unit // 6 + RAW_BUFS < NC:
+                    load_w(unit // 6 + RAW_BUFS)
+
+        def quants_after_run(r):
+            if r % 2 == 0:
+                w_quant(3 * (r // 2))
+            else:
+                w_quant(3 * (r // 2) + 1)
+                w_quant(3 * (r // 2) + 2)
+
+        def warm_pe(n):
+            for i in range(n):
+                nc.tensor.matmul(out=wb[3][:], lhsT=ones_b[:], rhs=wrow[:, 0:512], start=True, stop=True)
+
+        def preload_rsqrt():
+            nc.scalar.activation(out=warm2[:], in_=eps_t[:], func=ACT.Abs_reciprocal_sqrt)
+
+        for a in range(NA):
+            x_square(a)
+        h_make(0)
+        h_make(1)
+        sin_tables()
+        w_tables()
+        warm_pe(5)
+        t_units(range(0, 3))
+        warm_pe(3)
+        for unit in range(0, 3):
+            w_copy(unit, "s")
+        h_transpose(0)
+        warm_pe(3)
+        h_make(2)
+        h_make(3)
+        for g in range(NG):
+            h_copy(0, g, "s")
+        quants_after_run(0)
+        for g in range(NG):
+            h_quant(0, g)
+        t_units(range(3, 6))
+        warm_pe(3)
+        for unit in range(3, 6):
+            w_copy(unit, "s")
+        quants_after_run(1)
+        preload_rsqrt()
+        h_transpose(1)
+        mx(0)
+        mx(1)
+        for g in range(NG):
+            h_copy(1, g, "v")
+        for g in range(NG):
+            h_quant(1, g)
+        t_units(range(6, 9))
+
+        NPAIR = NC * NA // 2
+        NRUN = 2 * NC
+        SPLIT_FROM = NRUN - 4
+        for m in range(NRUN - 3):
+            r = m + 3
+            out_tile(m)
+            if m == 0:
+                head_squares(0)
+                head_squares(1)
+                head_rsqrt(0)
+                head_rsqrt(1)
+                for unit in range(6, 9):
+                    w_copy(unit, "s")
+                t_units(range(9, 12))
+                for unit in range(9, 12):
+                    w_copy(unit, "s")
+                rope_products(0)
+                w_quant(3)
+                rope_products(1)
+                w_quant(4)
+                w_quant(5)
+            else:
+                mx(2 * m)
+                t_units((3 * r, 3 * r + 1))
+                mx(2 * m + 1)
+                t_units((3 * r + 2,))
+                head_squares(2 * m)
+                w_copy(3 * r, "s")
+                head_rsqrt(2 * m)
+                rope_products(2 * m)
+                if m >= SPLIT_FROM:
+                    rope_add(m, 0, 1, nc.gpsimd)
+                    store(m, 0, 1)
+                if r % 2 == 1:
+                    w_quant(3 * (r // 2) + 1)
+                head_squares(2 * m + 1)
+                w_copy(3 * r + 1, "s")
+                head_rsqrt(2 * m + 1)
+                w_copy(3 * r + 2, "s")
+                rope_products(2 * m + 1)
+                w_quant(3 * (r // 2) + (2 if r % 2 == 1 else 0))
+            if m >= SPLIT_FROM:
+                rope_add(m, 1, 2, nc.gpsimd)
+                store(m, 1, 2)
+            else:
+                rope_add(m, 0, 2, nc.gpsimd)
+                store(m, 0, 2)
+
+        m = NRUN - 3
+        mx(2 * m)
+        mx(2 * m + 1)
+        mx(2 * m + 2)
+        mx(2 * m + 3)
+        for pair in (m, m + 1, m + 2):
+            out_tile(pair)
+        head_squares(2 * m)
+        head_squares(2 * m + 1)
+        head_rsqrt(2 * m)
+        head_rsqrt(2 * m + 1)
+        rope_products(2 * m)
+        rope_add(m, 0, 1, nc.vector)
+        store(m, 0, 1)
+        v_copy(2 * m + 2, "s")
+        v_copy(2 * m + 3, "s")
+        store(m + 1, 0, 2)
+        mx(2 * m + 4)
+        mx(2 * m + 5)
+        rope_products(2 * m + 1)
+        rope_add(m, 1, 2, nc.vector)
+        store(m, 1, 2)
+        v_copy(2 * m + 4, "s")
+        v_copy(2 * m + 5, "s")
+        store(m + 2, 0, 2)

@@ -25,7 +25,10 @@ ROPE_BASE = 1000000.0
 EPS = 1e-6
 TWO_PI = 2.0 * math.pi
 RAW_BUFS = 5
+CODE_BUFS = 5
 MANUAL = True
+
+UNITS = [(c, i % 3, i // 3) if c < 2 else (c, i // 2, i % 2) for c in range(NC) for i in range(6)]
 
 FLOPS = 2 * S * E * (NC * 512)
 
@@ -36,12 +39,12 @@ def tile_selectivetransformerlayer_pa_kernel(
     nc = tc.nc
     with ExitStack() as ctx:
         const = ctx.enter_context(tc.tile_pool(name="const", bufs=1))
-        rawp = ctx.enter_context(tc.tile_pool(name="rawp", bufs=RAW_BUFS))
-        codep = ctx.enter_context(tc.tile_pool(name="codep", bufs=3))
-        grp = ctx.enter_context(tc.tile_pool(name="grp", bufs=3))
+        rawp = ctx.enter_context(tc.tile_pool(name="rawp", bufs=2 * RAW_BUFS))
+        codep = ctx.enter_context(tc.tile_pool(name="codep", bufs=CODE_BUFS))
+        grp = ctx.enter_context(tc.tile_pool(name="grp", bufs=4))
         small = ctx.enter_context(tc.tile_pool(name="small", bufs=4))
         ep = ctx.enter_context(tc.tile_pool(name="ep", bufs=3))
-        outp = ctx.enter_context(tc.tile_pool(name="outp", bufs=4))
+        outp = ctx.enter_context(tc.tile_pool(name="outp", bufs=6))
         psum_t = ctx.enter_context(tc.psum_pool(name="psum_t", bufs=4))
         psum_a = ctx.enter_context(tc.psum_pool(name="psum_a", bufs=4))
         if MANUAL:
@@ -71,7 +74,7 @@ def tile_selectivetransformerlayer_pa_kernel(
             return o0_v[:, 4 * c : 4 * c + 4, cols]
 
         wrow = const.tile([P, E + 2 * D], BF16)
-        nc.vector.memset(wrow[:], 0.0)
+        nc.vector.memset(wrow[:].bitcast(U32), 0)
         ones_b = const.tile([P, P], BF16)
         nc.vector.memset(ones_b[:], 1.0)
         warm = const.tile([P, 1], F32)
@@ -93,19 +96,16 @@ def tile_selectivetransformerlayer_pa_kernel(
         raw = {}
 
         def load_w(c):
-            w_raw = rawp.tile([P, 4, E], BF16, tag="w_raw")
-            nc.sync.dma_start(out=w_raw[:], in_=w_src(c))
-            raw[c] = w_raw
+            for b in range(2):
+                w_raw = rawp.tile([P, 2, E], BF16, tag="w_raw")
+                nc.sync.dma_start(out=w_raw[:], in_=w_src(c)[:, 2 * b : 2 * b + 2, :])
+                raw[(c, b)] = w_raw
 
         for c in range(RAW_BUFS):
             load_w(c)
 
         tpos_i = const.tile([P, NA], I32)
         nc.gpsimd.iota(tpos_i[:], pattern=[[1, NA]], base=0, channel_multiplier=NA)
-        ident_f = const.tile([P, P], F32)
-        make_identity(nc, ident_f[:])
-        ident_b = const.tile([P, P], BF16)
-        make_identity(nc, ident_b[:])
         warm2 = const.tile([P, 1], F32)
         nc.scalar.activation(out=warm2[:], in_=warm[:], func=ACT.Sin)
 
@@ -118,6 +118,8 @@ def tile_selectivetransformerlayer_pa_kernel(
             else:
                 cj = ROPE_BASE ** (-2.0 * (j - 24) / 40.0) / TWO_PI
             nc.vector.tensor_scalar_mul(out=turns[:, 1, j, :], in0=tpos[:], scalar1=cj)
+        ident_f = const.tile([P, P], F32)
+        make_identity(nc, ident_f[:])
         nc.vector.tensor_scalar_add(out=turns[:, 0], in0=turns[:, 1], scalar1=0.25)
         NT = 2 * NF * NA
         turns_f = turns[:].rearrange("p s j a -> p (s j a)")
@@ -127,18 +129,9 @@ def tile_selectivetransformerlayer_pa_kernel(
         nc.vector.tensor_copy(out=whole[:], in_=whole_i[:])
         frac = const.tile([P, NT], F32)
         nc.vector.tensor_tensor(out=frac[:], in0=turns_f, in1=whole[:], op=ALU.subtract)
-        fneg = const.tile([P, NT], F32)
+        fneg = const.tile([P, 2, NF, NA], F32)
         nc.vector.scalar_tensor_tensor(
-            out=fneg[:], in0=frac[:], scalar=0.5, in1=frac[:], op0=ALU.is_gt, op1=ALU.subtract
-        )
-        fr = const.tile([P, 2, NF, NA], F32)
-        nc.vector.scalar_tensor_tensor(
-            out=fr[:].rearrange("p s j a -> p (s j a)"),
-            in0=fneg[:],
-            scalar=0.5,
-            in1=fneg[:],
-            op0=ALU.is_gt,
-            op1=ALU.subtract,
+            out=fneg[:].rearrange("p s j a -> p (s j a)"), in0=frac[:], scalar=0.5, in1=frac[:], op0=ALU.is_gt, op1=ALU.subtract
         )
 
         wb = []
@@ -153,7 +146,7 @@ def tile_selectivetransformerlayer_pa_kernel(
         nc.vector.tensor_copy(out=wqk[:], in_=wb[3][:, 0 : 2 * D])
 
         h = const.tile([P, NA, E], BF16)
-        junk = const.tile([P, E], BF16)
+        junk = const.tile([P, 2, E], BF16)
         ssx = const.tile([P, NA], F32)
         msx = const.tile([P, NA], F32)
         rx = const.tile([P, NA], F32)
@@ -162,7 +155,7 @@ def tile_selectivetransformerlayer_pa_kernel(
 
         def x_square(a):
             nc.scalar.activation(
-                out=junk[:], in_=x_sb[:, a, :], func=ACT.Square, accum_out=ssx[:, a : a + 1]
+                out=junk[:, a % 2, :], in_=x_sb[:, a, :], func=ACT.Square, accum_out=ssx[:, a : a + 1]
             )
             nc.gpsimd.tensor_scalar(
                 out=msx[:, a : a + 1],
@@ -179,34 +172,41 @@ def tile_selectivetransformerlayer_pa_kernel(
         def h_make(a):
             for g in range(NG):
                 sl = slice(g * 512, (g + 1) * 512)
-                nc.vector.scalar_tensor_tensor(
-                    out=h[:, a, sl].rearrange("p (t q) -> p t q", t=4),
-                    in0=x_sb[:, a, sl].rearrange("p (q t) -> p t q", t=4),
-                    scalar=rx[:, a : a + 1],
-                    in1=wb[g][:].rearrange("p (q t) -> p t q", t=4),
-                    op0=ALU.mult,
-                    op1=ALU.mult,
-                )
+                for u in range(2):
+                    lo = g * 512 + u * 256
+                    nc.vector.scalar_tensor_tensor(
+                        out=h[:, a, lo : lo + 256].rearrange("p (q e) -> p q e", e=2),
+                        in0=x_sb[:, a, sl].rearrange("p (q u e) -> p u q e", u=2, e=2)[:, u],
+                        scalar=rx[:, a : a + 1],
+                        in1=wb[g][:].rearrange("p (q u e) -> p u q e", u=2, e=2)[:, u],
+                        op0=ALU.mult,
+                        op1=ALU.mult,
+                    )
 
         hts = {}
         hgs = {}
 
         def h_transpose(pr):
             for g in range(NG):
-                ht = psum_t.tile([P, 2, 4, P], BF16, tag="tp")
+                ht = psum_t.tile([P, 2, 2 * P], F32, tag="tp")
                 for i in range(2):
-                    for t4 in range(4):
-                        lo = (4 * g + t4) * P
-                        nc.tensor.transpose(ht[:, i, t4, :], h[:, 2 * pr + i, lo : lo + P], ident_b[:])
+                    for u in range(2):
+                        lo = 256 * g + 128 * u
+                        nc.tensor.transpose(
+                            ht[:, u, i * P : (i + 1) * P],
+                            h[:, 2 * pr + i, :].bitcast(F32)[:, lo : lo + P],
+                            ident_f[:],
+                        )
                 hts[(pr, g)] = ht
 
         def h_copy(pr, g, eng):
-            hg = grp.tile([P, 2, P, 4], BF16, tag="hg", align_bytes=64)
-            src = hts[(pr, g)][:].rearrange("p i t r -> p i r t")
+            hg = grp.tile([P, 1024], BF16, tag="hg", align_bytes=64)
+            dst = hg[:].bitcast(F32).rearrange("p (n u) -> p n u", u=2)
+            src = hts[(pr, g)][:].rearrange("p u n -> p n u")
             if eng == "s":
-                nc.scalar.copy(out=hg[:], in_=src)
+                nc.scalar.copy(out=dst, in_=src)
             else:
-                nc.vector.tensor_copy(out=hg[:], in_=src)
+                nc.vector.tensor_copy(out=dst, in_=src)
             hgs[(pr, g)] = hg
 
         def h_quant(pr, g):
@@ -214,7 +214,7 @@ def tile_selectivetransformerlayer_pa_kernel(
             nc.vector.quantize_mx(
                 out=h_codes[:, g, cols].bitcast(FP8X4),
                 scales=h_scales[:, g, cols],
-                in_=hgs[(pr, g)][:].rearrange("p i r t -> p (i r t)"),
+                in_=hgs[(pr, g)][:],
             )
 
         cos_t = const.tile([P, NA, D], F32)
@@ -233,12 +233,12 @@ def tile_selectivetransformerlayer_pa_kernel(
             for dst, s, d0, d1, j0, j1, r, sign in pieces:
                 nc.scalar.activation(
                     out=dst[:, :, d0:d1].rearrange("p a (r j) -> p a r j", r=r),
-                    in_=fr[:, s, j0:j1, :]
+                    in_=fneg[:, s, j0:j1, :]
                     .rearrange("p j a -> p a j")
                     .unsqueeze(2)
                     .to_broadcast([P, NA, r, j1 - j0]),
                     func=ACT.Sin,
-                    scale=sign * TWO_PI,
+                    scale=-sign * TWO_PI,
                 )
 
         def w_tables():
@@ -272,24 +272,24 @@ def tile_selectivetransformerlayer_pa_kernel(
         wcodes = {}
 
         def w_transpose(unit):
-            c, g, bp = unit // 6, (unit % 6) // 2, unit % 2
+            c, g, bp = UNITS[unit]
             wt = psum_t.tile([P, 2, 256], F32, tag="tp")
             for bl in range(2):
                 for u in range(2):
                     lo = 256 * g + u
                     nc.tensor.transpose(
                         wt[:, u, bl * P : (bl + 1) * P],
-                        raw[c][:, 2 * bp + bl, :].bitcast(F32)[:, lo : 256 * (g + 1) : 2],
+                        raw[(c, bp)][:, bl, :].bitcast(F32)[:, lo : 256 * (g + 1) : 2],
                         ident_f[:],
                     )
             wts[unit] = wt
 
         def w_copy(unit, eng):
-            bp = unit % 2
+            c, g, bp = UNITS[unit]
             if bp == 0:
                 wg = grp.tile([P, 2048], BF16, tag="wg", align_bytes=64)
-                wgs[unit // 2] = wg
-            wg32 = wgs[unit // 2][:].bitcast(F32).rearrange("p (n u) -> p n u", u=2)
+                wgs[3 * c + g] = wg
+            wg32 = wgs[3 * c + g][:].bitcast(F32).rearrange("p (n u) -> p n u", u=2)
             dst = wg32[:, bp * 256 : (bp + 1) * 256, :]
             src = wts[unit][:].rearrange("p u n -> p n u")
             if eng == "s":
@@ -299,7 +299,7 @@ def tile_selectivetransformerlayer_pa_kernel(
 
         def w_quant(tile_no):
             c, g = tile_no // 3, tile_no % 3
-            if g == 0:
+            if c not in wcodes:
                 codes = codep.tile([P, NG, 512], U32, tag="codes", align_bytes=64)
                 scales = codep.tile([P, NG, 512], U8, tag="scales", align_bytes=64)
                 wcodes[c] = (codes, scales)
@@ -427,111 +427,97 @@ def tile_selectivetransformerlayer_pa_kernel(
         def preload_rsqrt():
             nc.scalar.activation(out=warm2[:], in_=eps_t[:], func=ACT.Abs_reciprocal_sqrt)
 
+        PAIRS = list(range(18))
+        U0 = 9
+        NT = 17
+
+        def units_until(i):
+            if i < 0:
+                return U0
+            return min(60, U0 - ((i + 1) * (U0 - 60) // NT))
+
+        pend = []
+
+        def copy_u(u, eng):
+            w_copy(u, eng)
+            c, g, bp = UNITS[u]
+            if bp == 1:
+                pend.append(3 * c + g)
+
+        def quant_pend(n=99):
+            while pend and n > 0:
+                w_quant(pend.pop(0))
+                n -= 1
+
         for a in range(NA):
             x_square(a)
+        sin_tables()
         h_make(0)
         h_make(1)
-        sin_tables()
-        w_tables()
-        warm_pe(5)
-        t_units(range(0, 3))
-        warm_pe(3)
-        for unit in range(0, 3):
-            w_copy(unit, "s")
+        t_units(range(0, 1))
         h_transpose(0)
-        warm_pe(3)
+        copy_u(0, "s")
+        t_units(range(1, 4))
         h_make(2)
         h_make(3)
-        for g in range(NG):
-            h_copy(0, g, "s")
-        quants_after_run(0)
+        h_copy(0, 0, "s")
+        h_copy(0, 1, "s")
+        h_copy(0, 2, "v")
+        w_tables()
+        for u in range(1, 4):
+            copy_u(u, "s")
+        t_units(range(4, 6))
         for g in range(NG):
             h_quant(0, g)
-        t_units(range(3, 6))
-        warm_pe(3)
-        for unit in range(3, 6):
-            w_copy(unit, "s")
-        quants_after_run(1)
-        preload_rsqrt()
         h_transpose(1)
-        mx(0)
-        mx(1)
-        for g in range(NG):
-            h_copy(1, g, "v")
+        copy_u(4, "s")
+        copy_u(5, "s")
+        h_copy(1, 0, "v")
+        quant_pend()
+        h_copy(1, 1, "s")
+        h_copy(1, 2, "s")
+        preload_rsqrt()
         for g in range(NG):
             h_quant(1, g)
-        t_units(range(6, 9))
 
-        NPAIR = NC * NA // 2
-        NRUN = 2 * NC
-        SPLIT_FROM = NRUN - 4
-        for m in range(NRUN - 3):
-            r = m + 3
+        for i, m in enumerate(PAIRS):
             out_tile(m)
-            if m == 0:
-                head_squares(0)
-                head_squares(1)
-                head_rsqrt(0)
-                head_rsqrt(1)
-                for unit in range(6, 9):
-                    w_copy(unit, "s")
-                t_units(range(9, 12))
-                for unit in range(9, 12):
-                    w_copy(unit, "s")
-                rope_products(0)
-                w_quant(3)
-                rope_products(1)
-                w_quant(4)
-                w_quant(5)
-            else:
-                mx(2 * m)
-                t_units((3 * r, 3 * r + 1))
-                mx(2 * m + 1)
-                t_units((3 * r + 2,))
-                head_squares(2 * m)
-                w_copy(3 * r, "s")
-                head_rsqrt(2 * m)
-                rope_products(2 * m)
-                if m >= SPLIT_FROM:
-                    rope_add(m, 0, 1, nc.gpsimd)
-                    store(m, 0, 1)
-                if r % 2 == 1:
-                    w_quant(3 * (r // 2) + 1)
-                head_squares(2 * m + 1)
-                w_copy(3 * r + 1, "s")
-                head_rsqrt(2 * m + 1)
-                w_copy(3 * r + 2, "s")
-                rope_products(2 * m + 1)
-                w_quant(3 * (r // 2) + (2 if r % 2 == 1 else 0))
-            if m >= SPLIT_FROM:
-                rope_add(m, 1, 2, nc.gpsimd)
-                store(m, 1, 2)
-            else:
+            us = list(range(units_until(i - 1), units_until(i)))
+            s0, s1 = 2 * m, 2 * m + 1
+            mx(s0)
+            if i == 0:
+                t_units(range(6, U0))
+            mx(s1)
+            t_units(us)
+            head_squares(s0)
+            if i == 0:
+                for u in range(6, U0):
+                    copy_u(u, "s")
+            head_rsqrt(s0)
+            head_squares(s1)
+            if us:
+                copy_u(us[0], "s")
+            head_rsqrt(s1)
+            for u in us[1:]:
+                copy_u(u, "s")
+            rope_products(s0)
+            quant_pend(1)
+            rope_products(s1)
+            quant_pend()
+            if i < len(PAIRS) - 1:
                 rope_add(m, 0, 2, nc.gpsimd)
                 store(m, 0, 2)
-
-        m = NRUN - 3
-        mx(2 * m)
-        mx(2 * m + 1)
-        mx(2 * m + 2)
-        mx(2 * m + 3)
-        for pair in (m, m + 1, m + 2):
+            else:
+                rope_add(m, 0, 1, nc.gpsimd)
+                store(m, 0, 1)
+                rope_add(m, 1, 2, nc.vector)
+                store(m, 1, 2)
+        m = NC * NA // 2 - 2
+        for s in range(4):
+            mx(2 * m + s)
+        for pair in (m, m + 1):
             out_tile(pair)
-        head_squares(2 * m)
-        head_squares(2 * m + 1)
-        head_rsqrt(2 * m)
-        head_rsqrt(2 * m + 1)
-        rope_products(2 * m)
-        rope_add(m, 0, 1, nc.vector)
-        store(m, 0, 1)
-        v_copy(2 * m + 2, "s")
-        v_copy(2 * m + 3, "s")
-        store(m + 1, 0, 2)
-        mx(2 * m + 4)
-        mx(2 * m + 5)
-        rope_products(2 * m + 1)
-        rope_add(m, 1, 2, nc.vector)
-        store(m, 1, 2)
-        v_copy(2 * m + 4, "s")
-        v_copy(2 * m + 5, "s")
-        store(m + 2, 0, 2)
+        for pair in (m, m + 1):
+            v_copy(2 * pair, "s")
+            v_copy(2 * pair + 1, "s")
+            store(pair, 0, 2)

@@ -501,7 +501,6 @@ def tile_selectivetransformerlayer_pa_kernel(
             for u in us[1:]:
                 copy_u(u, "s")
             rope_products(s0)
-            quant_pend(1)
             rope_products(s1)
             quant_pend()
             if i < len(PAIRS) - 1:

@@ -25,7 +25,7 @@ ROPE_BASE = 1000000.0
 EPS = 1e-6
 TWO_PI = 2.0 * math.pi
 RAW_BUFS = 5
-CODE_BUFS = 5
+CODE_BUFS = 4
 MANUAL = True
 
 UNITS = [(c, i % 3, i // 3) if c < 2 else (c, i // 2, i % 2) for c in range(NC) for i in range(6)]
@@ -42,9 +42,10 @@ def tile_selectivetransformerlayer_pa_kernel(
         rawp = ctx.enter_context(tc.tile_pool(name="rawp", bufs=2 * RAW_BUFS))
         codep = ctx.enter_context(tc.tile_pool(name="codep", bufs=CODE_BUFS))
         grp = ctx.enter_context(tc.tile_pool(name="grp", bufs=4))
+        yp = ctx.enter_context(tc.tile_pool(name="yp", bufs=1))
         small = ctx.enter_context(tc.tile_pool(name="small", bufs=4))
         ep = ctx.enter_context(tc.tile_pool(name="ep", bufs=3))
-        outp = ctx.enter_context(tc.tile_pool(name="outp", bufs=6))
+        outp = ctx.enter_context(tc.tile_pool(name="outp", bufs=5))
         psum_t = ctx.enter_context(tc.psum_pool(name="psum_t", bufs=4))
         psum_a = ctx.enter_context(tc.psum_pool(name="psum_a", bufs=4))
         if MANUAL:
@@ -112,12 +113,17 @@ def tile_selectivetransformerlayer_pa_kernel(
         tpos = const.tile([P, NA], F32)
         nc.vector.tensor_copy(out=tpos[:], in_=tpos_i[:])
         turns = const.tile([P, 2, NF, NA], F32)
-        for j in range(NF):
-            if j < 24:
-                cj = ROPE_BASE ** (-2.0 * j / 48.0) / TWO_PI
-            else:
-                cj = ROPE_BASE ** (-2.0 * (j - 24) / 40.0) / TWO_PI
-            nc.vector.tensor_scalar_mul(out=turns[:, 1, j, :], in0=tpos[:], scalar1=cj)
+        for j0 in (0, 24):
+            nc.vector.tensor_scalar_mul(out=turns[:, 1, j0, :], in0=tpos[:], scalar1=1.0 / TWO_PI)
+        for k in range(5):
+            for j0, n in ((0, 24), (24, 20)):
+                w = 2**k
+                m = min(w, n - w)
+                nc.vector.tensor_scalar_mul(
+                    out=turns[:, 1, j0 + w : j0 + w + m, :],
+                    in0=turns[:, 1, j0 : j0 + m, :],
+                    scalar1=ROPE_BASE ** (-1.0 * w / n),
+                )
         ident_f = const.tile([P, P], F32)
         make_identity(nc, ident_f[:])
         nc.vector.tensor_scalar_add(out=turns[:, 0], in0=turns[:, 1], scalar1=0.25)
@@ -134,16 +140,22 @@ def tile_selectivetransformerlayer_pa_kernel(
             out=fneg[:].rearrange("p s j a -> p (s j a)"), in0=frac[:], scalar=0.5, in1=frac[:], op0=ALU.is_gt, op1=ALU.subtract
         )
 
-        wb = []
-        for i in range(4):
-            n = 512 if i < 3 else 2 * D
-            wbi = psum_a.tile([P, 512], F32, tag="acc", name="wb%d" % i)
-            nc.tensor.matmul(
-                out=wbi[:, 0:n], lhsT=ones_b[:], rhs=wrow[:, 512 * i : 512 * i + n], start=True, stop=True
-            )
-            wb.append(wbi)
-        wqk = const.tile([P, 2 * D], F32)
-        nc.vector.tensor_copy(out=wqk[:], in_=wb[3][:, 0 : 2 * D])
+        wall = const.tile([P, E + 2 * D], BF16)
+        wbs = []
+        for i in range(2):
+            n = 1024 if i == 0 else 512 + 2 * D
+            wb = psum_a.tile([P, 1024], BF16, tag="acc", name="wb")
+            wbs.append(wb)
+            for lo in range(0, n, 512):
+                hi = min(lo + 512, n)
+                nc.tensor.matmul(
+                    out=wb[:, lo:hi], lhsT=ones_b[:], rhs=wrow[:, 1024 * i + lo : 1024 * i + hi], start=True, stop=True
+                )
+        def wall_copy(i):
+            n = 1024 if i == 0 else 512 + 2 * D
+            nc.vector.tensor_copy(out=wall[:, 1024 * i : 1024 * i + n], in_=wbs[i][:, 0:n])
+
+        wqk = wall[:, E : E + 2 * D]
 
         h = const.tile([P, NA, E], BF16)
         junk = const.tile([P, 2, E], BF16)
@@ -157,6 +169,8 @@ def tile_selectivetransformerlayer_pa_kernel(
             nc.scalar.activation(
                 out=junk[:, a % 2, :], in_=x_sb[:, a, :], func=ACT.Square, accum_out=ssx[:, a : a + 1]
             )
+
+        def x_root(a):
             nc.gpsimd.tensor_scalar(
                 out=msx[:, a : a + 1],
                 in0=ssx[:, a : a + 1],
@@ -169,19 +183,41 @@ def tile_selectivetransformerlayer_pa_kernel(
                 out=rx[:, a : a + 1], in0=msx[:, a : a + 1], in1=neghalf[:], op=ALU.pow
             )
 
+        def words(ap, u):
+            return ap.rearrange("p (w u e) -> p u w e", u=2, e=2)[:, u]
+
         def h_make(a):
-            for g in range(NG):
-                sl = slice(g * 512, (g + 1) * 512)
-                for u in range(2):
-                    lo = g * 512 + u * 256
+            for u in range(2):
+                for i in range(2):
+                    n = 512 - 256 * i
+                    lo = 768 * u + 512 * i
                     nc.vector.scalar_tensor_tensor(
-                        out=h[:, a, lo : lo + 256].rearrange("p (q e) -> p q e", e=2),
-                        in0=x_sb[:, a, sl].rearrange("p (q u e) -> p u q e", u=2, e=2)[:, u],
+                        out=h[:, a, lo : lo + n].rearrange("p (w e) -> p w e", e=2),
+                        in0=words(x_sb[:, a, 1024 * i : 1024 * i + 2 * n], u),
                         scalar=rx[:, a : a + 1],
-                        in1=wb[g][:].rearrange("p (q u e) -> p u q e", u=2, e=2)[:, u],
+                        in1=words(wbs[i][:, 0 : 2 * n], u),
                         op0=ALU.mult,
                         op1=ALU.mult,
                     )
+
+        ys = {}
+
+        def h_weight(a):
+            y = yp.tile([P, E], F32, tag="y")
+            nc.gpsimd.tensor_tensor(out=y[:], in0=x_sb[:, a, :], in1=wall[:, 0:E], op=ALU.mult)
+            ys[a] = y
+
+        def h_scale(a):
+            y = ys[a]
+            for u in range(2):
+                nc.gpsimd.tensor_scalar(
+                    out=h[:, a, u * 768 : (u + 1) * 768].rearrange("p (w e) -> p w e", e=2),
+                    in0=words(y[:], u),
+                    scalar1=rx[:, a : a + 1],
+                    scalar2=0.0,
+                    op0=ALU.mult,
+                    op1=ALU.add,
+                )
 
         hts = {}
         hgs = {}
@@ -191,7 +227,7 @@ def tile_selectivetransformerlayer_pa_kernel(
                 ht = psum_t.tile([P, 2, 2 * P], F32, tag="tp")
                 for i in range(2):
                     for u in range(2):
-                        lo = 256 * g + 128 * u
+                        lo = 384 * u + 128 * g
                         nc.tensor.transpose(
                             ht[:, u, i * P : (i + 1) * P],
                             h[:, 2 * pr + i, :].bitcast(F32)[:, lo : lo + P],
@@ -217,54 +253,42 @@ def tile_selectivetransformerlayer_pa_kernel(
                 in_=hgs[(pr, g)][:],
             )
 
-        cos_t = const.tile([P, NA, D], F32)
-        sin_t = const.tile([P, NA, D], F32)
+        trig = const.tile([P, 2, NF, NA], F32)
         tabs = {}
 
         def sin_tables():
-            pieces = (
-                (cos_t, 0, 0, 48, 0, 24, 2, 1.0),
-                (cos_t, 0, 48, 128, 24, 44, 4, 1.0),
-                (sin_t, 1, 0, 48, 0, 24, 2, -1.0),
-                (sin_t, 1, 48, 64, 24, 40, 1, -1.0),
-                (sin_t, 1, 64, 68, 40, 44, 1, 1.0),
-                (sin_t, 1, 68, 128, 24, 44, 3, 1.0),
+            nc.scalar.activation(
+                out=trig[:].rearrange("p s j a -> p (s j a)"),
+                in_=fneg[:].rearrange("p s j a -> p (s j a)"),
+                func=ACT.Sin,
+                scale=-TWO_PI,
             )
-            for dst, s, d0, d1, j0, j1, r, sign in pieces:
-                nc.scalar.activation(
-                    out=dst[:, :, d0:d1].rearrange("p a (r j) -> p a r j", r=r),
-                    in_=fneg[:, s, j0:j1, :]
-                    .rearrange("p j a -> p a j")
-                    .unsqueeze(2)
-                    .to_broadcast([P, NA, r, j1 - j0]),
-                    func=ACT.Sin,
-                    scale=-sign * TWO_PI,
-                )
 
-        def w_tables():
-            for i, nm in enumerate(("q", "k")):
+        def w_tables(which):
+            pieces = (
+                (0, 0, 48, 0, 0, 2),
+                (0, 48, 80, 0, 24, 4),
+                (1, 0, 4, 1, 40, 1),
+                (1, 4, 60, 1, 24, 3),
+                (1, 64, 48, 1, 0, 2),
+                (1, 112, 16, 1, 24, 1),
+            )
+            for i, nm in which:
                 tab = const.tile([P, NA, 2, D], F32, name="tab_" + nm)
-                ta = tab[:, :, 0, :]
-                tb = tab[:, :, 1, :]
-                w0 = i * D
-                nc.gpsimd.tensor_tensor(
-                    out=ta,
-                    in0=cos_t[:],
-                    in1=wqk[:, w0 : w0 + D].unsqueeze(1).to_broadcast([P, NA, D]),
-                    op=ALU.mult,
-                )
-                nc.gpsimd.tensor_tensor(
-                    out=tb[:, :, 0:64],
-                    in0=sin_t[:, :, 64:128],
-                    in1=wqk[:, w0 : w0 + 64].unsqueeze(1).to_broadcast([P, NA, 64]),
-                    op=ALU.mult,
-                )
-                nc.gpsimd.tensor_tensor(
-                    out=tb[:, :, 64:128],
-                    in0=sin_t[:, :, 0:64],
-                    in1=wqk[:, w0 + 64 : w0 + D].unsqueeze(1).to_broadcast([P, NA, 64]),
-                    op=ALU.mult,
-                )
+                for half, d0, n, s, j0, r in pieces:
+                    nj = n // r
+                    nc.gpsimd.tensor_tensor(
+                        out=tab[:, :, half, d0 : d0 + n].rearrange("p a (r j) -> p a r j", r=r),
+                        in0=trig[:, s, j0 : j0 + nj, :]
+                        .rearrange("p j a -> p a j")
+                        .unsqueeze(2)
+                        .to_broadcast([P, NA, r, nj]),
+                        in1=wqk[:, i * D + d0 : i * D + d0 + n]
+                        .rearrange("p (r j) -> p r j", r=r)
+                        .unsqueeze(1)
+                        .to_broadcast([P, NA, r, nj]),
+                        op=ALU.mult,
+                    )
                 tabs[nm] = tab
 
         wts = {}
@@ -332,8 +356,10 @@ def tile_selectivetransformerlayer_pa_kernel(
 
         def head_squares(slot):
             acc = accs[slot]
-            ss = small.tile([P, 4], F32, tag="ss")
-            sss[slot] = ss
+            if slot % 2 == 0:
+                ss = small.tile([P, 8], F32, tag="ss")
+                sss[slot // 2] = ss
+            ss = sss[slot // 2][:, 4 * (slot % 2) : 4 * (slot % 2) + 4]
             for hh in range(4):
                 sq = small.tile([P, D], BF16, tag="sq")
                 nc.scalar.activation(
@@ -343,17 +369,17 @@ def tile_selectivetransformerlayer_pa_kernel(
                     accum_out=ss[:, hh : hh + 1],
                 )
 
-        def head_rsqrt(slot):
-            rs = small.tile([P, 4], F32, tag="rs")
+        def head_rsqrt(pair):
+            rs = small.tile([P, 8], F32, tag="rs")
             nc.scalar.activation(
-                out=rs[:], in_=sss[slot][:], func=ACT.Abs_reciprocal_sqrt, scale=1.0 / D, bias=eps_t[:]
+                out=rs[:], in_=sss[pair][:], func=ACT.Abs_reciprocal_sqrt, scale=1.0 / D, bias=eps_t[:]
             )
-            rss[slot] = rs
+            rss[pair] = rs
 
         def rope_products(slot):
             c, a = slot // NA, slot % NA
             acc = accs[slot]
-            rs = rss[slot]
+            rs = rss[slot // 2]
             tab = tabs["k" if c == NC - 2 else "q"]
             if slot % 2 == 0:
                 t12 = ep.tile([P, 4, 2, 2, D], F32, tag="t12")
@@ -363,7 +389,7 @@ def tile_selectivetransformerlayer_pa_kernel(
                 nc.vector.scalar_tensor_tensor(
                     out=t12[:, hh, slot % 2, :, :],
                     in0=acc[:, hh * D : (hh + 1) * D].unsqueeze(1).to_broadcast([P, 2, D]),
-                    scalar=rs[:, hh : hh + 1],
+                    scalar=rs[:, 4 * (slot % 2) + hh : 4 * (slot % 2) + hh + 1],
                     in1=tab[:, a, :, :],
                     op0=ALU.mult,
                     op1=ALU.mult,
@@ -382,7 +408,7 @@ def tile_selectivetransformerlayer_pa_kernel(
                 out=o[:, :, i0:i1, 0:64],
                 in0=t12[:, :, i0:i1, 0, 0:64],
                 in1=t12[:, :, i0:i1, 1, 64:128],
-                op=ALU.add,
+                op=ALU.subtract,
             )
             eng.tensor_tensor(
                 out=o[:, :, i0:i1, 64:128],
@@ -413,23 +439,12 @@ def tile_selectivetransformerlayer_pa_kernel(
                 if unit % 6 == 5 and unit // 6 + RAW_BUFS < NC:
                     load_w(unit // 6 + RAW_BUFS)
 
-        def quants_after_run(r):
-            if r % 2 == 0:
-                w_quant(3 * (r // 2))
-            else:
-                w_quant(3 * (r // 2) + 1)
-                w_quant(3 * (r // 2) + 2)
-
-        def warm_pe(n):
-            for i in range(n):
-                nc.tensor.matmul(out=wb[3][:], lhsT=ones_b[:], rhs=wrow[:, 0:512], start=True, stop=True)
-
         def preload_rsqrt():
             nc.scalar.activation(out=warm2[:], in_=eps_t[:], func=ACT.Abs_reciprocal_sqrt)
 
         PAIRS = list(range(18))
         U0 = 9
-        NT = 17
+        NT = 16
 
         def units_until(i):
             if i < 0:
@@ -449,34 +464,48 @@ def tile_selectivetransformerlayer_pa_kernel(
                 w_quant(pend.pop(0))
                 n -= 1
 
-        for a in range(NA):
-            x_square(a)
+        x_square(0)
+        x_root(0)
+        x_square(1)
+        x_root(1)
         sin_tables()
+        x_square(2)
+        x_root(2)
+        x_square(3)
         h_make(0)
+        wall_copy(0)
+        wall_copy(1)
+        h_weight(3)
+        x_root(3)
         h_make(1)
         t_units(range(0, 1))
         h_transpose(0)
+        t_units(range(1, 9))
         copy_u(0, "s")
-        t_units(range(1, 4))
-        h_make(2)
-        h_make(3)
         h_copy(0, 0, "s")
-        h_copy(0, 1, "s")
+        h_copy(0, 1, "v")
         h_copy(0, 2, "v")
-        w_tables()
-        for u in range(1, 4):
-            copy_u(u, "s")
-        t_units(range(4, 6))
+        h_make(2)
         for g in range(NG):
             h_quant(0, g)
-        h_transpose(1)
-        copy_u(4, "s")
-        copy_u(5, "s")
-        h_copy(1, 0, "v")
+        h_scale(3)
+        for u in range(1, 6):
+            copy_u(u, "s")
         quant_pend()
-        h_copy(1, 1, "s")
-        h_copy(1, 2, "s")
+        w_tables(((0, "q"),))
+        mx(0)
+        mx(1)
+        h_transpose(1)
         preload_rsqrt()
+        copy_u(6, "v")
+        copy_u(7, "v")
+        copy_u(8, "v")
+        head_squares(0)
+        head_squares(1)
+        h_copy(1, 0, "s")
+        h_copy(1, 1, "v")
+        h_copy(1, 2, "v")
+        head_rsqrt(0)
         for g in range(NG):
             h_quant(1, g)
 
@@ -484,25 +513,24 @@ def tile_selectivetransformerlayer_pa_kernel(
             out_tile(m)
             us = list(range(units_until(i - 1), units_until(i)))
             s0, s1 = 2 * m, 2 * m + 1
-            mx(s0)
-            if i == 0:
-                t_units(range(6, U0))
-            mx(s1)
+            if i > 0:
+                mx(s0)
+                mx(s1)
             t_units(us)
-            head_squares(s0)
-            if i == 0:
-                for u in range(6, U0):
-                    copy_u(u, "s")
-            head_rsqrt(s0)
-            head_squares(s1)
-            if us:
-                copy_u(us[0], "s")
-            head_rsqrt(s1)
-            for u in us[1:]:
+            if i > 0:
+                head_squares(s0)
+                head_squares(s1)
+            for n, u in enumerate(us):
+                if n == 1 and i > 0:
+                    head_rsqrt(m)
                 copy_u(u, "s")
+            if len(us) < 2 and i > 0:
+                head_rsqrt(m)
             rope_products(s0)
             rope_products(s1)
             quant_pend()
+            if i == 8:
+                w_tables(((1, "k"),))
             if i < len(PAIRS) - 1:
                 rope_add(m, 0, 2, nc.gpsimd)
                 store(m, 0, 2)

@@ -25,7 +25,7 @@ ROPE_BASE = 1000000.0
 EPS = 1e-6
 TWO_PI = 2.0 * math.pi
 RAW_BUFS = 5
-CODE_BUFS = 4
+CODE_BUFS = 5
 MANUAL = True
 
 UNITS = [(c, i % 3, i // 3) if c < 2 else (c, i // 2, i % 2) for c in range(NC) for i in range(6)]
@@ -42,10 +42,9 @@ def tile_selectivetransformerlayer_pa_kernel(
         rawp = ctx.enter_context(tc.tile_pool(name="rawp", bufs=2 * RAW_BUFS))
         codep = ctx.enter_context(tc.tile_pool(name="codep", bufs=CODE_BUFS))
         grp = ctx.enter_context(tc.tile_pool(name="grp", bufs=4))
-        yp = ctx.enter_context(tc.tile_pool(name="yp", bufs=1))
         small = ctx.enter_context(tc.tile_pool(name="small", bufs=4))
         ep = ctx.enter_context(tc.tile_pool(name="ep", bufs=3))
-        outp = ctx.enter_context(tc.tile_pool(name="outp", bufs=5))
+        outp = ctx.enter_context(tc.tile_pool(name="outp", bufs=6))
         psum_t = ctx.enter_context(tc.psum_pool(name="psum_t", bufs=4))
         psum_a = ctx.enter_context(tc.psum_pool(name="psum_a", bufs=4))
         if MANUAL:
@@ -140,7 +139,7 @@ def tile_selectivetransformerlayer_pa_kernel(
             out=fneg[:].rearrange("p s j a -> p (s j a)"), in0=frac[:], scalar=0.5, in1=frac[:], op0=ALU.is_gt, op1=ALU.subtract
         )
 
-        wall = const.tile([P, E + 2 * D], BF16)
+        wqk = const.tile([P, 2 * D], F32)
         wbs = []
         for i in range(2):
             n = 1024 if i == 0 else 512 + 2 * D
@@ -151,11 +150,7 @@ def tile_selectivetransformerlayer_pa_kernel(
                 nc.tensor.matmul(
                     out=wb[:, lo:hi], lhsT=ones_b[:], rhs=wrow[:, 1024 * i + lo : 1024 * i + hi], start=True, stop=True
                 )
-        def wall_copy(i):
-            n = 1024 if i == 0 else 512 + 2 * D
-            nc.vector.tensor_copy(out=wall[:, 1024 * i : 1024 * i + n], in_=wbs[i][:, 0:n])
-
-        wqk = wall[:, E : E + 2 * D]
+        nc.vector.tensor_copy(out=wqk[:], in_=wbs[1][:, 512 : 512 + 2 * D])
 
         h = const.tile([P, NA, E], BF16)
         junk = const.tile([P, 2, E], BF16)
@@ -200,25 +195,6 @@ def tile_selectivetransformerlayer_pa_kernel(
                         op1=ALU.mult,
                     )
 
-        ys = {}
-
-        def h_weight(a):
-            y = yp.tile([P, E], F32, tag="y")
-            nc.gpsimd.tensor_tensor(out=y[:], in0=x_sb[:, a, :], in1=wall[:, 0:E], op=ALU.mult)
-            ys[a] = y
-
-        def h_scale(a):
-            y = ys[a]
-            for u in range(2):
-                nc.gpsimd.tensor_scalar(
-                    out=h[:, a, u * 768 : (u + 1) * 768].rearrange("p (w e) -> p w e", e=2),
-                    in0=words(y[:], u),
-                    scalar1=rx[:, a : a + 1],
-                    scalar2=0.0,
-                    op0=ALU.mult,
-                    op1=ALU.add,
-                )
-
         hts = {}
         hgs = {}
 
@@ -253,40 +229,39 @@ def tile_selectivetransformerlayer_pa_kernel(
                 in_=hgs[(pr, g)][:],
             )
 
-        trig = const.tile([P, 2, NF, NA], F32)
+        cos_t = const.tile([P, NA, D], F32)
+        sin_t = const.tile([P, NA, D], F32)
         tabs = {}
 
         def sin_tables():
-            nc.scalar.activation(
-                out=trig[:].rearrange("p s j a -> p (s j a)"),
-                in_=fneg[:].rearrange("p s j a -> p (s j a)"),
-                func=ACT.Sin,
-                scale=-TWO_PI,
+            pieces = (
+                (cos_t, 0, 0, 48, 0, 24, 2),
+                (cos_t, 0, 48, 128, 24, 44, 4),
+                (sin_t, 1, 0, 48, 0, 24, 2),
+                (sin_t, 1, 48, 64, 24, 40, 1),
+                (sin_t, 1, 64, 68, 40, 44, 1),
+                (sin_t, 1, 68, 128, 24, 44, 3),
             )
+            for dst, s, d0, d1, j0, j1, r in pieces:
+                nc.scalar.activation(
+                    out=dst[:, :, d0:d1].rearrange("p a (r j) -> p a r j", r=r),
+                    in_=fneg[:, s, j0:j1, :]
+                    .rearrange("p j a -> p a j")
+                    .unsqueeze(2)
+                    .to_broadcast([P, NA, r, j1 - j0]),
+                    func=ACT.Sin,
+                    scale=-TWO_PI,
+                )
 
         def w_tables(which):
-            pieces = (
-                (0, 0, 48, 0, 0, 2),
-                (0, 48, 80, 0, 24, 4),
-                (1, 0, 4, 1, 40, 1),
-                (1, 4, 60, 1, 24, 3),
-                (1, 64, 48, 1, 0, 2),
-                (1, 112, 16, 1, 24, 1),
-            )
             for i, nm in which:
                 tab = const.tile([P, NA, 2, D], F32, name="tab_" + nm)
-                for half, d0, n, s, j0, r in pieces:
-                    nj = n // r
+                for half, d0, d1, src, s0 in ((0, 0, 128, cos_t, 0), (1, 0, 64, sin_t, 64), (1, 64, 128, sin_t, 0)):
+                    n = d1 - d0
                     nc.gpsimd.tensor_tensor(
-                        out=tab[:, :, half, d0 : d0 + n].rearrange("p a (r j) -> p a r j", r=r),
-                        in0=trig[:, s, j0 : j0 + nj, :]
-                        .rearrange("p j a -> p a j")
-                        .unsqueeze(2)
-                        .to_broadcast([P, NA, r, nj]),
-                        in1=wqk[:, i * D + d0 : i * D + d0 + n]
-                        .rearrange("p (r j) -> p r j", r=r)
-                        .unsqueeze(1)
-                        .to_broadcast([P, NA, r, nj]),
+                        out=tab[:, :, half, d0:d1],
+                        in0=src[:, :, s0 : s0 + n],
+                        in1=wqk[:, i * D + d0 : i * D + d1].unsqueeze(1).to_broadcast([P, NA, n]),
                         op=ALU.mult,
                     )
                 tabs[nm] = tab
@@ -401,9 +376,9 @@ def tile_selectivetransformerlayer_pa_kernel(
             o = outp.tile([P, 4, 2, D], F32, tag="o")
             outs[pair] = o
 
-        def rope_add(pair, i0, i1, eng):
-            t12 = prods[pair]
-            o = outs[pair]
+        def rope_add(pair, i0, i1, eng, h0=0, h1=4):
+            t12 = prods[pair][:, h0:h1]
+            o = outs[pair][:, h0:h1]
             eng.tensor_tensor(
                 out=o[:, :, i0:i1, 0:64],
                 in0=t12[:, :, i0:i1, 0, 0:64],
@@ -472,11 +447,9 @@ def tile_selectivetransformerlayer_pa_kernel(
         x_square(2)
         x_root(2)
         x_square(3)
-        h_make(0)
-        wall_copy(0)
-        wall_copy(1)
-        h_weight(3)
         x_root(3)
+        w_tables(((0, "q"), (1, "k")))
+        h_make(0)
         h_make(1)
         t_units(range(0, 1))
         h_transpose(0)
@@ -488,16 +461,15 @@ def tile_selectivetransformerlayer_pa_kernel(
         h_make(2)
         for g in range(NG):
             h_quant(0, g)
-        h_scale(3)
         for u in range(1, 6):
             copy_u(u, "s")
         quant_pend()
-        w_tables(((0, "q"),))
+        h_make(3)
         mx(0)
         mx(1)
         h_transpose(1)
         preload_rsqrt()
-        copy_u(6, "v")
+        copy_u(6, "s")
         copy_u(7, "v")
         copy_u(8, "v")
         head_squares(0)
@@ -529,10 +501,11 @@ def tile_selectivetransformerlayer_pa_kernel(
             rope_products(s0)
             rope_products(s1)
             quant_pend()
-            if i == 8:
-                w_tables(((1, "k"),))
             if i < len(PAIRS) - 1:
-                rope_add(m, 0, 2, nc.gpsimd)
+                hv = 3 if i % 3 == 1 else 4
+                rope_add(m, 0, 2, nc.gpsimd, 0, hv)
+                if hv < 4:
+                    rope_add(m, 0, 2, nc.vector, hv, 4)
                 store(m, 0, 2)
             else:
                 rope_add(m, 0, 1, nc.gpsimd)

@@ -25,7 +25,7 @@ ROPE_BASE = 1000000.0
 EPS = 1e-6
 TWO_PI = 2.0 * math.pi
 RAW_BUFS = 5
-CODE_BUFS = 5
+CODE_BUFS = 4
 MANUAL = True
 
 UNITS = [(c, i % 3, i // 3) if c < 2 else (c, i // 2, i % 2) for c in range(NC) for i in range(6)]
@@ -42,9 +42,10 @@ def tile_selectivetransformerlayer_pa_kernel(
         rawp = ctx.enter_context(tc.tile_pool(name="rawp", bufs=2 * RAW_BUFS))
         codep = ctx.enter_context(tc.tile_pool(name="codep", bufs=CODE_BUFS))
         grp = ctx.enter_context(tc.tile_pool(name="grp", bufs=4))
+        yp = ctx.enter_context(tc.tile_pool(name="yp", bufs=1))
         small = ctx.enter_context(tc.tile_pool(name="small", bufs=4))
         ep = ctx.enter_context(tc.tile_pool(name="ep", bufs=3))
-        outp = ctx.enter_context(tc.tile_pool(name="outp", bufs=6))
+        outp = ctx.enter_context(tc.tile_pool(name="outp", bufs=5))
         psum_t = ctx.enter_context(tc.psum_pool(name="psum_t", bufs=4))
         psum_a = ctx.enter_context(tc.psum_pool(name="psum_a", bufs=4))
         if MANUAL:
@@ -85,12 +86,11 @@ def tile_selectivetransformerlayer_pa_kernel(
         nc.vector.memset(neghalf[:], -0.5)
 
         x_sb = const.tile([P, NA, E], BF16)
-        for a in range(2):
-            nc.sync.dma_start(out=x_sb[:, a, :], in_=x_v[:, a, :])
+        nc.sync.dma_start(out=x_sb[:, 0, :], in_=x_v[:, 0, :])
         nc.sync.dma_start(out=wrow[0:1, 0:E], in_=ln1_w.unsqueeze(0))
         nc.sync.dma_start(out=wrow[0:1, E : E + D], in_=q_norm_w.unsqueeze(0))
         nc.sync.dma_start(out=wrow[0:1, E + D : E + 2 * D], in_=k_norm_w.unsqueeze(0))
-        for a in range(2, NA):
+        for a in range(1, NA):
             nc.sync.dma_start(out=x_sb[:, a, :], in_=x_v[:, a, :])
 
         raw = {}
@@ -139,7 +139,8 @@ def tile_selectivetransformerlayer_pa_kernel(
             out=fneg[:].rearrange("p s j a -> p (s j a)"), in0=frac[:], scalar=0.5, in1=frac[:], op0=ALU.is_gt, op1=ALU.subtract
         )
 
-        wqk = const.tile([P, 2 * D], F32)
+        wall = const.tile([P, E + 2 * D], BF16)
+        wqk = wall[:, E : E + 2 * D]
         wbs = []
         for i in range(2):
             n = 1024 if i == 0 else 512 + 2 * D
@@ -150,7 +151,10 @@ def tile_selectivetransformerlayer_pa_kernel(
                 nc.tensor.matmul(
                     out=wb[:, lo:hi], lhsT=ones_b[:], rhs=wrow[:, 1024 * i + lo : 1024 * i + hi], start=True, stop=True
                 )
-        nc.vector.tensor_copy(out=wqk[:], in_=wbs[1][:, 512 : 512 + 2 * D])
+
+        def wall_copy(i):
+            n = 1024 if i == 0 else 512 + 2 * D
+            nc.vector.tensor_copy(out=wall[:, 1024 * i : 1024 * i + n], in_=wbs[i][:, 0:n])
 
         h = const.tile([P, NA, E], BF16)
         junk = const.tile([P, 2, E], BF16)
@@ -178,22 +182,29 @@ def tile_selectivetransformerlayer_pa_kernel(
                 out=rx[:, a : a + 1], in0=msx[:, a : a + 1], in1=neghalf[:], op=ALU.pow
             )
 
-        def words(ap, u):
-            return ap.rearrange("p (w u e) -> p u w e", u=2, e=2)[:, u]
-
         def h_make(a):
-            for u in range(2):
-                for i in range(2):
-                    n = 512 - 256 * i
-                    lo = 768 * u + 512 * i
-                    nc.vector.scalar_tensor_tensor(
-                        out=h[:, a, lo : lo + n].rearrange("p (w e) -> p w e", e=2),
-                        in0=words(x_sb[:, a, 1024 * i : 1024 * i + 2 * n], u),
-                        scalar=rx[:, a : a + 1],
-                        in1=words(wbs[i][:, 0 : 2 * n], u),
-                        op0=ALU.mult,
-                        op1=ALU.mult,
-                    )
+            for i in range(2):
+                n = 1024 - 512 * i
+                nc.vector.scalar_tensor_tensor(
+                    out=h[:, a, 1024 * i : 1024 * i + n],
+                    in0=x_sb[:, a, 1024 * i : 1024 * i + n],
+                    scalar=rx[:, a : a + 1],
+                    in1=wbs[i][:, 0:n],
+                    op0=ALU.mult,
+                    op1=ALU.mult,
+                )
+
+        ys = {}
+
+        def h_weight(a):
+            y = yp.tile([P, E], F32, tag="y")
+            nc.gpsimd.tensor_tensor(out=y[:], in0=x_sb[:, a, :], in1=wall[:, 0:E], op=ALU.mult)
+            ys[a] = y
+
+        def h_scale(a):
+            nc.gpsimd.tensor_scalar(
+                out=h[:, a, :], in0=ys[a][:], scalar1=rx[:, a : a + 1], scalar2=0.0, op0=ALU.mult, op1=ALU.add
+            )
 
         hts = {}
         hgs = {}
@@ -203,10 +214,10 @@ def tile_selectivetransformerlayer_pa_kernel(
                 ht = psum_t.tile([P, 2, 2 * P], F32, tag="tp")
                 for i in range(2):
                     for u in range(2):
-                        lo = 384 * u + 128 * g
+                        lo = 256 * g + u
                         nc.tensor.transpose(
                             ht[:, u, i * P : (i + 1) * P],
-                            h[:, 2 * pr + i, :].bitcast(F32)[:, lo : lo + P],
+                            h[:, 2 * pr + i, :].bitcast(F32)[:, lo : 256 * (g + 1) : 2],
                             ident_f[:],
                         )
                 hts[(pr, g)] = ht
@@ -417,9 +428,9 @@ def tile_selectivetransformerlayer_pa_kernel(
         def preload_rsqrt():
             nc.scalar.activation(out=warm2[:], in_=eps_t[:], func=ACT.Abs_reciprocal_sqrt)
 
-        PAIRS = list(range(18))
+        PAIRS = list(range(20))
         U0 = 9
-        NT = 16
+        NT = 17
 
         def units_until(i):
             if i < 0:
@@ -445,15 +456,19 @@ def tile_selectivetransformerlayer_pa_kernel(
         x_root(1)
         sin_tables()
         x_square(2)
-        x_root(2)
         x_square(3)
+        wall_copy(0)
+        wall_copy(1)
+        h_weight(3)
+        x_root(2)
         x_root(3)
-        w_tables(((0, "q"), (1, "k")))
         h_make(0)
         h_make(1)
         t_units(range(0, 1))
         h_transpose(0)
-        t_units(range(1, 9))
+        t_units(range(1, 6))
+        h_scale(3)
+        w_tables(((0, "q"),))
         copy_u(0, "s")
         h_copy(0, 0, "s")
         h_copy(0, 1, "v")
@@ -464,45 +479,59 @@ def tile_selectivetransformerlayer_pa_kernel(
         for u in range(1, 6):
             copy_u(u, "s")
         quant_pend()
-        h_make(3)
+        w_tables(((1, "k"),))
+        h_transpose(1)
+
         mx(0)
         mx(1)
-        h_transpose(1)
+
+        t_units(range(6, 9))
         preload_rsqrt()
-        copy_u(6, "s")
-        copy_u(7, "v")
-        copy_u(8, "v")
-        head_squares(0)
-        head_squares(1)
-        h_copy(1, 0, "s")
+        h_copy(1, 0, "v")
         h_copy(1, 1, "v")
         h_copy(1, 2, "v")
+
+
+        head_squares(0)
+        head_squares(1)
+        copy_u(6, "s")
         head_rsqrt(0)
+        copy_u(7, "s")
+        copy_u(8, "s")
         for g in range(NG):
             h_quant(1, g)
 
+        todo = []
         for i, m in enumerate(PAIRS):
             out_tile(m)
             us = list(range(units_until(i - 1), units_until(i)))
             s0, s1 = 2 * m, 2 * m + 1
+            v_pair = m >= 18
             if i > 0:
                 mx(s0)
                 mx(s1)
             t_units(us)
-            if i > 0:
+            if v_pair:
+                v_copy(s0, "s")
+                v_copy(s1, "v" if m == 19 else "s")
+            elif i > 0:
                 head_squares(s0)
                 head_squares(s1)
             for n, u in enumerate(us):
-                if n == 1 and i > 0:
+                if n == 1 and i > 0 and not v_pair:
                     head_rsqrt(m)
                 copy_u(u, "s")
-            if len(us) < 2 and i > 0:
+            if len(us) < 2 and i > 0 and not v_pair:
                 head_rsqrt(m)
-            rope_products(s0)
-            rope_products(s1)
+            if not v_pair:
+                rope_products(s0)
+                rope_products(s1)
             quant_pend()
-            if i < len(PAIRS) - 1:
-                hv = 3 if i % 3 == 1 else 4
+            if v_pair:
+                store(m, 0, 1)
+                store(m, 1, 2)
+            elif m < 17:
+                hv = 4
                 rope_add(m, 0, 2, nc.gpsimd, 0, hv)
                 if hv < 4:
                     rope_add(m, 0, 2, nc.vector, hv, 4)
@@ -512,12 +541,3 @@ def tile_selectivetransformerlayer_pa_kernel(
                 store(m, 0, 1)
                 rope_add(m, 1, 2, nc.vector)
                 store(m, 1, 2)
-        m = NC * NA // 2 - 2
-        for s in range(4):
-            mx(2 * m + s)
-        for pair in (m, m + 1):
-            out_tile(pair)
-        for pair in (m, m + 1):
-            v_copy(2 * pair, "s")
-            v_copy(2 * pair + 1, "s")
-            store(pair, 0, 2)

@@ -342,10 +342,8 @@ def tile_selectivetransformerlayer_pa_kernel(
 
         def head_squares(slot):
             acc = accs[slot]
-            if slot % 2 == 0:
-                ss = small.tile([P, 8], F32, tag="ss")
-                sss[slot // 2] = ss
-            ss = sss[slot // 2][:, 4 * (slot % 2) : 4 * (slot % 2) + 4]
+            ss = small.tile([P, 4], F32, tag="ss")
+            sss[slot] = ss
             for hh in range(4):
                 sq = small.tile([P, D], BF16, tag="sq")
                 nc.scalar.activation(
@@ -355,17 +353,17 @@ def tile_selectivetransformerlayer_pa_kernel(
                     accum_out=ss[:, hh : hh + 1],
                 )
 
-        def head_rsqrt(pair):
-            rs = small.tile([P, 8], F32, tag="rs")
+        def head_rsqrt(slot):
+            rs = small.tile([P, 4], F32, tag="rs")
             nc.scalar.activation(
-                out=rs[:], in_=sss[pair][:], func=ACT.Abs_reciprocal_sqrt, scale=1.0 / D, bias=eps_t[:]
+                out=rs[:], in_=sss[slot][:], func=ACT.Abs_reciprocal_sqrt, scale=1.0 / D, bias=eps_t[:]
             )
-            rss[pair] = rs
+            rss[slot] = rs
 
         def rope_products(slot):
             c, a = slot // NA, slot % NA
             acc = accs[slot]
-            rs = rss[slot // 2]
+            rs = rss[slot]
             tab = tabs["k" if c == NC - 2 else "q"]
             if slot % 2 == 0:
                 t12 = ep.tile([P, 4, 2, 2, D], F32, tag="t12")
@@ -375,7 +373,7 @@ def tile_selectivetransformerlayer_pa_kernel(
                 nc.vector.scalar_tensor_tensor(
                     out=t12[:, hh, slot % 2, :, :],
                     in0=acc[:, hh * D : (hh + 1) * D].unsqueeze(1).to_broadcast([P, 2, D]),
-                    scalar=rs[:, 4 * (slot % 2) + hh : 4 * (slot % 2) + hh + 1],
+                    scalar=rs[:, hh : hh + 1],
                     in1=tab[:, a, :, :],
                     op0=ALU.mult,
                     op1=ALU.mult,
@@ -496,6 +494,7 @@ def tile_selectivetransformerlayer_pa_kernel(
         head_squares(1)
         copy_u(6, "s")
         head_rsqrt(0)
+        head_rsqrt(1)
         copy_u(7, "s")
         copy_u(8, "s")
         for g in range(NG):
@@ -516,13 +515,13 @@ def tile_selectivetransformerlayer_pa_kernel(
                 v_copy(s1, "v" if m == 19 else "s")
             elif i > 0:
                 head_squares(s0)
+                head_rsqrt(s0)
                 head_squares(s1)
-            for n, u in enumerate(us):
-                if n == 1 and i > 0 and not v_pair:
-                    head_rsqrt(m)
+                for u in us[:1]:
+                    copy_u(u, "s")
+                head_rsqrt(s1)
+            for u in us[1:] if i > 0 and not v_pair else us:
                 copy_u(u, "s")
-            if len(us) < 2 and i > 0 and not v_pair:
-                head_rsqrt(m)
             if not v_pair:
                 rope_products(s0)
                 rope_products(s1)

import math
from contextlib import ExitStack

import concourse.mybir as mybir
from concourse.masks import make_identity

F32 = mybir.dt.float32
BF16 = mybir.dt.bfloat16
I32 = mybir.dt.int32
U32 = mybir.dt.uint32
U8 = mybir.dt.uint8
FP8X4 = mybir.dt.float8_e4m3fn_x4
ACT = mybir.ActivationFunctionType
ALU = mybir.AluOpType

P = 128
S = 512
E = 1536
D = 128
NA = S // P
NG = E // 512
NC = 10
NF = 44
ROPE_BASE = 1000000.0
EPS = 1e-6
TWO_PI = 2.0 * math.pi
RAW_BUFS = 5
CODE_BUFS = 4
MANUAL = True

UNITS = [(c, i % 3, i // 3) if c < 2 else (c, i // 2, i % 2) for c in range(NC) for i in range(6)]

FLOPS = 2 * S * E * (NC * 512)


def tile_selectivetransformerlayer_pa_kernel(
    tc, x, ln1_w, wq, wk, wv, q_norm_w, k_norm_w, out_0, out_1, out_2
):
    nc = tc.nc
    with ExitStack() as ctx:
        const = ctx.enter_context(tc.tile_pool(name="const", bufs=1))
        rawp = ctx.enter_context(tc.tile_pool(name="rawp", bufs=2 * RAW_BUFS))
        codep = ctx.enter_context(tc.tile_pool(name="codep", bufs=CODE_BUFS))
        grp = ctx.enter_context(tc.tile_pool(name="grp", bufs=4))
        yp = ctx.enter_context(tc.tile_pool(name="yp", bufs=1))
        small = ctx.enter_context(tc.tile_pool(name="small", bufs=4))
        ep = ctx.enter_context(tc.tile_pool(name="ep", bufs=3))
        outp = ctx.enter_context(tc.tile_pool(name="outp", bufs=5))
        psum_t = ctx.enter_context(tc.psum_pool(name="psum_t", bufs=4))
        psum_a = ctx.enter_context(tc.psum_pool(name="psum_a", bufs=4))
        if MANUAL:
            ctx.enter_context(tc.manual_schedule())

        x_v = x.rearrange("o (p a) k -> p (o a) k", a=NA)
        wq_v = wq.rearrange("(c b p) k -> c p b k", b=4, p=P)
        wk_v = wk.rearrange("(b p) k -> p b k", p=P)
        wv_v = wv.rearrange("(b p) k -> p b k", p=P)
        o0_v = out_0.rearrange("o h (p a) d -> p (o h) (a d)", a=NA)
        o1_v = out_1.rearrange("o h (p a) d -> p (o h) (a d)", a=NA)
        o2_v = out_2.rearrange("o h (p a) d -> p (o h) (a d)", a=NA)

        def w_src(c):
            if c == NC - 1:
                return wv_v
            if c == NC - 2:
                return wk_v
            return wq_v[c]

        def o_dst(c, a0, a1):
            cols = slice(a0 * D, a1 * D)
            if c == NC - 1:
                return o2_v[:, :, cols]
            if c == NC - 2:
                return o1_v[:, :, cols]
            return o0_v[:, 4 * c : 4 * c + 4, cols]

        wrow = const.tile([P, E + 2 * D], BF16)
        nc.vector.memset(wrow[:].bitcast(U32), 0)
        ones_b = const.tile([P, P], BF16)
        nc.vector.memset(ones_b[:], 1.0)
        warm = const.tile([P, 1], F32)
        nc.vector.memset(warm[:], 0.0)
        eps_t = const.tile([P, 1], F32)
        nc.vector.memset(eps_t[:], EPS)
        neghalf = const.tile([P, 1], F32)
        nc.vector.memset(neghalf[:], -0.5)

        x_sb = const.tile([P, NA, E], BF16)
        nc.sync.dma_start(out=x_sb[:, 0, :], in_=x_v[:, 0, :])
        nc.sync.dma_start(out=wrow[0:1, 0:E], in_=ln1_w.unsqueeze(0))
        nc.sync.dma_start(out=wrow[0:1, E : E + D], in_=q_norm_w.unsqueeze(0))
        nc.sync.dma_start(out=wrow[0:1, E + D : E + 2 * D], in_=k_norm_w.unsqueeze(0))
        for a in range(1, NA):
            nc.sync.dma_start(out=x_sb[:, a, :], in_=x_v[:, a, :])

        raw = {}

        def load_w(c):
            for b in range(2):
                w_raw = rawp.tile([P, 2, E], BF16, tag="w_raw")
                nc.sync.dma_start(out=w_raw[:], in_=w_src(c)[:, 2 * b : 2 * b + 2, :])
                raw[(c, b)] = w_raw

        for c in range(RAW_BUFS):
            load_w(c)

        tpos_i = const.tile([P, NA], I32)
        nc.gpsimd.iota(tpos_i[:], pattern=[[1, NA]], base=0, channel_multiplier=NA)
        warm2 = const.tile([P, 1], F32)
        nc.scalar.activation(out=warm2[:], in_=warm[:], func=ACT.Sin)

        tpos = const.tile([P, NA], F32)
        nc.vector.tensor_copy(out=tpos[:], in_=tpos_i[:])
        turns = const.tile([P, 2, NF, NA], F32)
        for j0 in (0, 24):
            nc.vector.tensor_scalar_mul(out=turns[:, 1, j0, :], in0=tpos[:], scalar1=1.0 / TWO_PI)
        for k in range(5):
            for j0, n in ((0, 24), (24, 20)):
                w = 2**k
                m = min(w, n - w)
                nc.vector.tensor_scalar_mul(
                    out=turns[:, 1, j0 + w : j0 + w + m, :],
                    in0=turns[:, 1, j0 : j0 + m, :],
                    scalar1=ROPE_BASE ** (-1.0 * w / n),
                )
        ident_f = const.tile([P, P], F32)
        make_identity(nc, ident_f[:])
        nc.vector.tensor_scalar_add(out=turns[:, 0], in0=turns[:, 1], scalar1=0.25)
        NT = 2 * NF * NA
        turns_f = turns[:].rearrange("p s j a -> p (s j a)")
        whole_i = const.tile([P, NT], I32)
        nc.vector.tensor_copy(out=whole_i[:], in_=turns_f)
        whole = const.tile([P, NT], F32)
        nc.vector.tensor_copy(out=whole[:], in_=whole_i[:])
        frac = const.tile([P, NT], F32)
        nc.vector.tensor_tensor(out=frac[:], in0=turns_f, in1=whole[:], op=ALU.subtract)
        fneg = const.tile([P, 2, NF, NA], F32)
        nc.vector.scalar_tensor_tensor(
            out=fneg[:].rearrange("p s j a -> p (s j a)"), in0=frac[:], scalar=0.5, in1=frac[:], op0=ALU.is_gt, op1=ALU.subtract
        )

        wall = const.tile([P, E + 2 * D], BF16)
        wqk = wall[:, E : E + 2 * D]
        wbs = []
        for i in range(2):
            n = 1024 if i == 0 else 512 + 2 * D
            wb = psum_a.tile([P, 1024], BF16, tag="acc", name="wb")
            wbs.append(wb)
            for lo in range(0, n, 512):
                hi = min(lo + 512, n)
                nc.tensor.matmul(
                    out=wb[:, lo:hi], lhsT=ones_b[:], rhs=wrow[:, 1024 * i + lo : 1024 * i + hi], start=True, stop=True
                )

        def wall_copy(i):
            n = 1024 if i == 0 else 512 + 2 * D
            nc.vector.tensor_copy(out=wall[:, 1024 * i : 1024 * i + n], in_=wbs[i][:, 0:n])

        h = const.tile([P, NA, E], BF16)
        junk = const.tile([P, 2, E], BF16)
        ssx = const.tile([P, NA], F32)
        msx = const.tile([P, NA], F32)
        rx = const.tile([P, NA], F32)
        h_codes = const.tile([P, NG, S], U32, align_bytes=64)
        h_scales = const.tile([P, NG, S], U8, align_bytes=64)

        def x_square(a):
            nc.scalar.activation(
                out=junk[:, a % 2, :], in_=x_sb[:, a, :], func=ACT.Square, accum_out=ssx[:, a : a + 1]
            )

        def x_root(a):
            nc.gpsimd.tensor_scalar(
                out=msx[:, a : a + 1],
                in0=ssx[:, a : a + 1],
                scalar1=1.0 / E,
                scalar2=EPS,
                op0=ALU.mult,
                op1=ALU.add,
            )
            nc.gpsimd.tensor_tensor(
                out=rx[:, a : a + 1], in0=msx[:, a : a + 1], in1=neghalf[:], op=ALU.pow
            )

        def h_make(a):
            for i in range(2):
                n = 1024 - 512 * i
                nc.vector.scalar_tensor_tensor(
                    out=h[:, a, 1024 * i : 1024 * i + n],
                    in0=x_sb[:, a, 1024 * i : 1024 * i + n],
                    scalar=rx[:, a : a + 1],
                    in1=wbs[i][:, 0:n],
                    op0=ALU.mult,
                    op1=ALU.mult,
                )

        ys = {}

        def h_weight(a):
            y = yp.tile([P, E], F32, tag="y")
            nc.gpsimd.tensor_tensor(out=y[:], in0=x_sb[:, a, :], in1=wall[:, 0:E], op=ALU.mult)
            ys[a] = y

        def h_scale(a):
            nc.gpsimd.tensor_scalar(
                out=h[:, a, :], in0=ys[a][:], scalar1=rx[:, a : a + 1], scalar2=0.0, op0=ALU.mult, op1=ALU.add
            )

        hts = {}
        hgs = {}

        def h_transpose(pr):
            for g in range(NG):
                ht = psum_t.tile([P, 2, 2 * P], F32, tag="tp")
                for i in range(2):
                    for u in range(2):
                        lo = 256 * g + u
                        nc.tensor.transpose(
                            ht[:, u, i * P : (i + 1) * P],
                            h[:, 2 * pr + i, :].bitcast(F32)[:, lo : 256 * (g + 1) : 2],
                            ident_f[:],
                        )
                hts[(pr, g)] = ht

        def h_copy(pr, g, eng):
            hg = grp.tile([P, 1024], BF16, tag="hg", align_bytes=64)
            dst = hg[:].bitcast(F32).rearrange("p (n u) -> p n u", u=2)
            src = hts[(pr, g)][:].rearrange("p u n -> p n u")
            if eng == "s":
                nc.scalar.copy(out=dst, in_=src)
            else:
                nc.vector.tensor_copy(out=dst, in_=src)
            hgs[(pr, g)] = hg

        def h_quant(pr, g):
            cols = slice(pr * 256, (pr + 1) * 256)
            nc.vector.quantize_mx(
                out=h_codes[:, g, cols].bitcast(FP8X4),
                scales=h_scales[:, g, cols],
                in_=hgs[(pr, g)][:],
            )

        cos_t = const.tile([P, NA, D], F32)
        sin_t = const.tile([P, NA, D], F32)
        tabs = {}

        def sin_tables():
            pieces = (
                (cos_t, 0, 0, 48, 0, 24, 2),
                (cos_t, 0, 48, 128, 24, 44, 4),
                (sin_t, 1, 0, 48, 0, 24, 2),
                (sin_t, 1, 48, 64, 24, 40, 1),
                (sin_t, 1, 64, 68, 40, 44, 1),
                (sin_t, 1, 68, 128, 24, 44, 3),
            )
            for dst, s, d0, d1, j0, j1, r in pieces:
                nc.scalar.activation(
                    out=dst[:, :, d0:d1].rearrange("p a (r j) -> p a r j", r=r),
                    in_=fneg[:, s, j0:j1, :]
                    .rearrange("p j a -> p a j")
                    .unsqueeze(2)
                    .to_broadcast([P, NA, r, j1 - j0]),
                    func=ACT.Sin,
                    scale=-TWO_PI,
                )

        def w_tables(which):
            for i, nm in which:
                tab = const.tile([P, NA, 2, D], F32, name="tab_" + nm)
                for half, d0, d1, src, s0 in ((0, 0, 128, cos_t, 0), (1, 0, 64, sin_t, 64), (1, 64, 128, sin_t, 0)):
                    n = d1 - d0
                    nc.gpsimd.tensor_tensor(
                        out=tab[:, :, half, d0:d1],
                        in0=src[:, :, s0 : s0 + n],
                        in1=wqk[:, i * D + d0 : i * D + d1].unsqueeze(1).to_broadcast([P, NA, n]),
                        op=ALU.mult,
                    )
                tabs[nm] = tab

        wts = {}
        wgs = {}
        wcodes = {}

        def w_transpose(unit):
            c, g, bp = UNITS[unit]
            wt = psum_t.tile([P, 2, 256], F32, tag="tp")
            for bl in range(2):
                for u in range(2):
                    lo = 256 * g + u
                    nc.tensor.transpose(
                        wt[:, u, bl * P : (bl + 1) * P],
                        raw[(c, bp)][:, bl, :].bitcast(F32)[:, lo : 256 * (g + 1) : 2],
                        ident_f[:],
                    )
            wts[unit] = wt

        def w_copy(unit, eng):
            c, g, bp = UNITS[unit]
            if bp == 0:
                wg = grp.tile([P, 2048], BF16, tag="wg", align_bytes=64)
                wgs[3 * c + g] = wg
            wg32 = wgs[3 * c + g][:].bitcast(F32).rearrange("p (n u) -> p n u", u=2)
            dst = wg32[:, bp * 256 : (bp + 1) * 256, :]
            src = wts[unit][:].rearrange("p u n -> p n u")
            if eng == "s":
                nc.scalar.copy(out=dst, in_=src)
            else:
                nc.vector.tensor_copy(out=dst, in_=src)

        def w_quant(tile_no):
            c, g = tile_no // 3, tile_no % 3
            if c not in wcodes:
                codes = codep.tile([P, NG, 512], U32, tag="codes", align_bytes=64)
                scales = codep.tile([P, NG, 512], U8, tag="scales", align_bytes=64)
                wcodes[c] = (codes, scales)
            codes, scales = wcodes[c]
            nc.vector.quantize_mx(
                out=codes[:, g, :].bitcast(FP8X4), scales=scales[:, g, :], in_=wgs[tile_no][:]
            )

        accs = {}
        rss = {}
        prods = {}

        def mx(slot):
            c, a = slot // NA, slot % NA
            codes, scales = wcodes[c]
            acc = psum_a.tile([P, 512], F32, tag="acc")
            for g in range(NG):
                nc.tensor.matmul_mx(
                    out=acc[:],
                    lhsT=h_codes[:, g, a * P : (a + 1) * P].bitcast(FP8X4),
                    lhsT_scale=h_scales[:, g, a * P : (a + 1) * P],
                    rhs=codes[:, g, :].bitcast(FP8X4),
                    rhs_scale=scales[:, g, :],
                    start=(g == 0),
                    stop=(g == NG - 1),
                )
            accs[slot] = acc

        sss = {}

        def head_squares(slot):
            acc = accs[slot]
            ss = small.tile([P, 4], F32, tag="ss")
            sss[slot] = ss
            for hh in range(4):
                sq = small.tile([P, D], BF16, tag="sq")
                nc.scalar.activation(
                    out=sq[:],
                    in_=acc[:, hh * D : (hh + 1) * D],
                    func=ACT.Square,
                    accum_out=ss[:, hh : hh + 1],
                )

        def head_rsqrt(slot):
            rs = small.tile([P, 4], F32, tag="rs")
            nc.scalar.activation(
                out=rs[:], in_=sss[slot][:], func=ACT.Abs_reciprocal_sqrt, scale=1.0 / D, bias=eps_t[:]
            )
            rss[slot] = rs

        def rope_products(slot):
            c, a = slot // NA, slot % NA
            acc = accs[slot]
            rs = rss[slot]
            tab = tabs["k" if c == NC - 2 else "q"]
            if slot % 2 == 0:
                t12 = ep.tile([P, 4, 2, 2, D], F32, tag="t12")
                prods[slot // 2] = t12
            t12 = prods[slot // 2]
            for hh in range(4):
                nc.vector.scalar_tensor_tensor(
                    out=t12[:, hh, slot % 2, :, :],
                    in0=acc[:, hh * D : (hh + 1) * D].unsqueeze(1).to_broadcast([P, 2, D]),
                    scalar=rs[:, hh : hh + 1],
                    in1=tab[:, a, :, :],
                    op0=ALU.mult,
                    op1=ALU.mult,
                )

        outs = {}

        def out_tile(pair):
            o = outp.tile([P, 4, 2, D], F32, tag="o")
            outs[pair] = o

        def rope_add(pair, i0, i1, eng, h0=0, h1=4):
            t12 = prods[pair][:, h0:h1]
            o = outs[pair][:, h0:h1]
            eng.tensor_tensor(
                out=o[:, :, i0:i1, 0:64],
                in0=t12[:, :, i0:i1, 0, 0:64],
                in1=t12[:, :, i0:i1, 1, 64:128],
                op=ALU.subtract,
            )
            eng.tensor_tensor(
                out=o[:, :, i0:i1, 64:128],
                in0=t12[:, :, i0:i1, 0, 64:128],
                in1=t12[:, :, i0:i1, 1, 0:64],
                op=ALU.add,
            )

        def store(pair, i0, i1):
            c, a = (2 * pair) // NA, (2 * pair) % NA
            src = outs[pair]
            if i1 - i0 == 2:
                nc.sync.dma_start(out=o_dst(c, a, a + 2), in_=src[:].rearrange("p h i d -> p h (i d)"))
            else:
                nc.sync.dma_start(out=o_dst(c, a + i0, a + i1), in_=src[:, :, i0, :])

        def v_copy(slot, eng):
            dst = outs[slot // 2][:, :, slot % 2, :]
            src = accs[slot][:].rearrange("p (h d) -> p h d", d=D)
            if eng == "s":
                nc.scalar.copy(out=dst, in_=src)
            else:
                nc.vector.tensor_copy(out=dst, in_=src)

        def t_units(units):
            for unit in units:
                w_transpose(unit)
                if unit % 6 == 5 and unit // 6 + RAW_BUFS < NC:
                    load_w(unit // 6 + RAW_BUFS)

        def preload_rsqrt():
            nc.scalar.activation(out=warm2[:], in_=eps_t[:], func=ACT.Abs_reciprocal_sqrt)

        PAIRS = list(range(20))
        U0 = 9
        NT = 17

        def units_until(i):
            if i < 0:
                return U0
            return min(60, U0 - ((i + 1) * (U0 - 60) // NT))

        pend = []

        def copy_u(u, eng):
            w_copy(u, eng)
            c, g, bp = UNITS[u]
            if bp == 1:
                pend.append(3 * c + g)

        def quant_pend(n=99):
            while pend and n > 0:
                w_quant(pend.pop(0))
                n -= 1

        x_square(0)
        x_root(0)
        x_square(1)
        x_root(1)
        sin_tables()
        x_square(2)
        x_square(3)
        wall_copy(0)
        wall_copy(1)
        h_weight(3)
        x_root(2)
        x_root(3)
        h_make(0)
        h_make(1)
        t_units(range(0, 1))
        h_transpose(0)
        t_units(range(1, 6))
        h_scale(3)
        w_tables(((0, "q"),))
        copy_u(0, "s")
        h_copy(0, 0, "s")
        h_copy(0, 1, "v")
        h_copy(0, 2, "v")
        h_make(2)
        for g in range(NG):
            h_quant(0, g)
        for u in range(1, 6):
            copy_u(u, "s")
        quant_pend()
        w_tables(((1, "k"),))
        h_transpose(1)

        mx(0)
        mx(1)

        t_units(range(6, 9))
        preload_rsqrt()
        h_copy(1, 0, "v")
        h_copy(1, 1, "v")
        h_copy(1, 2, "v")


        head_squares(0)
        head_squares(1)
        copy_u(6, "s")
        head_rsqrt(0)
        head_rsqrt(1)
        copy_u(7, "s")
        copy_u(8, "s")
        for g in range(NG):
            h_quant(1, g)

        todo = []
        for i, m in enumerate(PAIRS):
            out_tile(m)
            us = list(range(units_until(i - 1), units_until(i)))
            s0, s1 = 2 * m, 2 * m + 1
            v_pair = m >= 18
            if i > 0:
                mx(s0)
                mx(s1)
            t_units(us)
            if v_pair:
                v_copy(s0, "s")
                v_copy(s1, "v" if m == 19 else "s")
            elif i > 0:
                head_squares(s0)
                head_rsqrt(s0)
                head_squares(s1)
                for u in us[:1]:
                    copy_u(u, "s")
                head_rsqrt(s1)
            for u in us[1:] if i > 0 and not v_pair else us:
                copy_u(u, "s")
            if not v_pair:
                rope_products(s0)
                rope_products(s1)
            quant_pend()
            if v_pair:
                store(m, 0, 1)
                store(m, 1, 2)
            elif m < 17:
                hv = 4
                rope_add(m, 0, 2, nc.gpsimd, 0, hv)
                if hv < 4:
                    rope_add(m, 0, 2, nc.vector, hv, 4)
                store(m, 0, 2)
            else:
                rope_add(m, 0, 1, nc.gpsimd)
                store(m, 0, 1)
                rope_add(m, 1, 2, nc.vector)
                store(m, 1, 2)
